import numpy as np
import ml_dtypes


def mxq(x, axis, fmt="e4m3"):
    dtype, down = {"e4m3": (ml_dtypes.float8_e4m3fn, 7), "e5m2": (ml_dtypes.float8_e5m2, 14)}[fmt]
    v = np.moveaxis(np.asarray(x, np.float32).astype(ml_dtypes.bfloat16).astype(np.float64), axis, -1)
    blocks = v.reshape(v.shape[:-1] + (-1, 32))
    amax = np.abs(blocks).max(-1, keepdims=True)
    byte = np.maximum(np.where(amax > 0, np.frexp(amax)[1] - 1 + 127, 0) - down, 1)
    scale = np.exp2(byte - 127.0)
    codes = (blocks / scale).astype(np.float32).astype(dtype).astype(np.float64)
    return np.moveaxis((codes * scale).reshape(v.shape), -1, axis)


WIDE = False


def mx_kscale(k):
    if not WIDE:
        return np.ones(k)
    levels = np.array([10, -10, 5, -5, 0])
    a = np.random.permutation(np.resize(levels, k // 512 * 4)).reshape(k // 512, 4)
    idx = np.arange(k)
    return np.exp2(a[idx // 512, idx % 128 // 32])


BF16 = ml_dtypes.bfloat16


def bf(x):
    return np.asarray(x, np.float32).astype(BF16)


def f64(x):
    return np.asarray(x).astype(np.float64)


E2M1 = np.array([0.0, 0.5, 1.0, 1.5, 2.0, 3.0, 4.0, 6.0, -0.0, -0.5, -1.0, -1.5, -2.0, -3.0, -4.0, -6.0])


def pack_weight(w, fmt):
    k, n = w.shape
    w = f64(bf(w)).reshape(k // 32, 32, n)
    amax = np.abs(w).max(1)
    if fmt == "e4m3":
        byte = np.frexp(amax)[1] - 1 + 127 - 7
    else:
        mant, ex = np.frexp(amax / 6.0)
        byte = np.where(mant > 0.5, ex, ex - 1) + 127
    byte = np.clip(np.where(amax > 0, byte, 1), 1, 254)
    scaled = (w * np.exp2(127.0 - byte)[:, None, :]).reshape(k, n).astype(np.float32)
    by_word = np.ascontiguousarray(scaled.reshape(k // 512, 128, 4, n).transpose(0, 1, 3, 2))
    if fmt == "e4m3":
        words = by_word.astype(ml_dtypes.float8_e4m3fn).view(np.uint8)
    else:
        c = by_word.astype(ml_dtypes.float4_e2m1fn).view(np.uint8) & 0xF
        words = c[..., 0::2] | (c[..., 1::2] << 4)
    return np.ascontiguousarray(words), np.ascontiguousarray(byte.astype(np.uint8).reshape(k // 512, 16, n))


def unpack_weight(words, scales, fmt):
    g, p, n, _ = words.shape
    if fmt == "e4m3":
        vals = np.ascontiguousarray(words).view(ml_dtypes.float8_e4m3fn).astype(np.float64)
    else:
        nib = np.empty((g, p, n, 4), np.uint8)
        nib[..., 0::2] = words & 0xF
        nib[..., 1::2] = words >> 4
        vals = E2M1[nib]
    vals = vals * np.repeat(np.exp2(scales.astype(np.float64) - 127.0), 8, axis=1)[..., None]
    return vals.transpose(0, 1, 3, 2).reshape(g * 512, n)


B, SY, SX, D, F = 2, 512, 2048, 512, 2048
EPS = 1e-5
FMT = "e4m3"


def layer_norm_all(t):
    mu = t.mean()
    var = np.square(t - mu).mean()
    return (t - mu) / np.sqrt(var + EPS)


def setup_inputs():
    t = mx_kscale(F)
    h2 = bf(np.random.standard_normal((B, SY, D)))
    w_ff1 = np.random.standard_normal((F, D)) / np.sqrt(D) * t[:, None]
    w_ff1_words, w_ff1_scales = pack_weight(np.ascontiguousarray(w_ff1.T), FMT)
    b_ff1 = bf(np.random.standard_normal(F) * 0.3 * t)
    w_ff2 = np.random.standard_normal((D, F)) * 1.4 / np.sqrt(F) / t[None, :]
    w_ff2_words, w_ff2_scales = pack_weight(np.ascontiguousarray(w_ff2.T), FMT)
    b_ff2 = bf(0.2 + 0.2 * np.random.standard_normal(D))
    return {"h2": h2,
            "w_ff1_words": w_ff1_words,
            "w_ff1_scales": w_ff1_scales,
            "b_ff1": b_ff1,
            "w_ff2_words": w_ff2_words,
            "w_ff2_scales": w_ff2_scales,
            "b_ff2": b_ff2}


def reference(h2, w_ff1_words, w_ff1_scales, b_ff1, w_ff2_words, w_ff2_scales, b_ff2):
    h = f64(h2)
    a = np.maximum((mxq(h, 2, "e4m3") @ unpack_weight(w_ff1_words, w_ff1_scales, FMT)) + f64(b_ff1), 0.0)
    ff = (mxq(a, 2, "e4m3") @ unpack_weight(w_ff2_words, w_ff2_scales, FMT)) + f64(b_ff2)
    return layer_norm_all(h + ff)

@@ -1,0 +1,279 @@
+from contextlib import ExitStack
+
+import concourse.mybir as mybir
+from concourse.masks import make_identity
+
+F32 = mybir.dt.float32
+BF16 = mybir.dt.bfloat16
+I32 = mybir.dt.int32
+U32 = mybir.dt.uint32
+U8 = mybir.dt.uint8
+FP8X4 = mybir.dt.float8_e4m3fn_x4
+ALU = mybir.AluOpType
+ACT = mybir.ActivationFunctionType
+
+P = 128
+K_PASS = 4 * P
+TOKENS = 1024
+D_MODEL = 512
+D_FF = 2048
+EPS = 1e-5
+N_TILES = TOKENS // P
+N_GROUPS = D_FF // K_PASS
+PAIR = 2
+N_PAIRS = N_TILES // PAIR
+QUADRANTS = 4
+
+FLOPS = 2 * TOKENS * D_MODEL * D_FF * 2
+
+
+def block(index, width):
+    return slice(index * width, (index + 1) * width)
+
+
+def tile_decoderblock_pb_kernel(
+    tc, h2, w_ff1_words, w_ff1_scales, b_ff1, w_ff2_words, w_ff2_scales, b_ff2, out
+):
+    nc = tc.nc
+    h_rows = h2.flatten_outer_dims().rearrange("(p i) d -> p i d", i=N_TILES)
+    out_rows = out.flatten_outer_dims().rearrange("(p i) d -> p i d", i=N_TILES)
+
+    with ExitStack() as ctx:
+        keep = ctx.enter_context(tc.tile_pool(name="keep", bufs=1))
+        ring = ctx.enter_context(tc.tile_pool(name="ring", bufs=2))
+        psum_x = ctx.enter_context(tc.psum_pool(name="psum_x", bufs=4))
+        psum_a = ctx.enter_context(tc.psum_pool(name="psum_a", bufs=2))
+        psum_h = ctx.enter_context(tc.psum_pool(name="psum_h", bufs=1))
+        psum_o = ctx.enter_context(tc.psum_pool(name="psum_o", bufs=1))
+        ctx.enter_context(tc.manual_schedule())
+
+        identity = keep.tile([P, P], F32)
+        mean_weights = keep.tile([P, P], F32)
+        eps = keep.tile([P, 1], F32)
+        table_warmer = keep.tile([P, 1], F32)
+        h_sb = keep.tile([P, N_TILES, D_MODEL], BF16)
+        h_grouped = keep.tile([P, N_TILES * K_PASS], BF16, align_bytes=64)
+        h_words = keep.tile([P, TOKENS], U32, align_bytes=64)
+        h_scales = keep.tile([P, TOKENS], U8, align_bytes=64)
+        w1_words = keep.tile([P, D_FF], U32, align_bytes=64)
+        w1_scales = keep.tile([P, D_FF], U8, align_bytes=64)
+        w2_words = keep.tile([P, N_GROUPS, D_MODEL], U32, align_bytes=64)
+        w2_scales = keep.tile([P, N_GROUPS, D_MODEL], U8, align_bytes=64)
+        b1_all = keep.tile([P, D_FF], BF16)
+        b2_all = keep.tile([P, D_MODEL], BF16)
+        h_plus_b2 = keep.tile([P, N_TILES, D_MODEL], F32)
+        t_sb = keep.tile([P, N_TILES, D_MODEL], F32)
+        squares = keep.tile([P, D_MODEL], BF16)
+        t_sum = keep.tile([P, N_TILES], F32)
+        t_sq = keep.tile([P, N_TILES], F32)
+        moments = keep.tile([P, 2], F32)
+        minus_var = keep.tile([P, 1], F32)
+        std = keep.tile([P, 1], F32)
+        rstd = keep.tile([P, 1], F32)
+        shift = keep.tile([P, 1], F32)
+
+        nc.vector.memset(w1_scales[:].bitcast(I32), 0)
+        nc.vector.memset(w2_scales[:].bitcast(I32), 0)
+        nc.vector.memset(eps[:], EPS)
+        nc.vector.memset(mean_weights[:], 1.0 / (TOKENS * D_MODEL))
+
+        def load_h(pair):
+            tiles = block(pair, PAIR)
+            nc.sync.dma_start(out=h_sb[:, tiles, :], in_=h_rows[:, tiles, :])
+
+        load_h(0)
+        for quad in range(QUADRANTS):
+            nc.sync.dma_start(
+                out=w1_scales[32 * quad : 32 * quad + 4, :].bitcast(I32),
+                in_=w_ff1_scales[0, 4 * quad : 4 * quad + 4, :].bitcast(I32),
+            )
+        w1_dram = w_ff1_words[0].rearrange("p n t -> p (n t)").bitcast(I32)
+        for g in range(N_GROUPS):
+            nc.sync.dma_start(
+                out=w1_words[:, block(g, K_PASS)].bitcast(I32), in_=w1_dram[:, block(g, K_PASS)]
+            )
+        load_h(1)
+        load_h(2)
+        for quad in range(QUADRANTS):
+            nc.sync.dma_start(
+                out=w2_scales[32 * quad : 32 * quad + 4, :, :].bitcast(I32),
+                in_=w_ff2_scales[:, 4 * quad : 4 * quad + 4, :]
+                .bitcast(I32)
+                .rearrange("g r n -> r g n"),
+            )
+        for g in range(N_GROUPS):
+            nc.sync.dma_start(
+                out=w2_words[:, g, :].bitcast(I32),
+                in_=w_ff2_words[g].rearrange("p n t -> p (n t)").bitcast(I32),
+            )
+        load_h(3)
+
+        nc.gpsimd.dma_start(out=b1_all[:], in_=b_ff1.partition_broadcast(P))
+        make_identity(nc, identity[:])
+        nc.gpsimd.dma_start(out=b2_all[:], in_=b_ff2.partition_broadcast(P))
+        for i in range(N_TILES):
+            nc.gpsimd.tensor_tensor(
+                out=h_plus_b2[:, i, :], in0=h_sb[:, i, :], in1=b2_all[:], op=ALU.add
+            )
+
+        nc.scalar.activation(out=table_warmer[:], in_=eps[:], func=ACT.Sqrt)
+
+        def quantise_h(pair):
+            bank = psum_h.tile([P, 2, PAIR * P], F32, name="h_bank", tag="psum_h")
+            for j in range(PAIR):
+                words = h_sb[:, PAIR * pair + j, :].bitcast(F32)
+                for u in range(2):
+                    nc.tensor.transpose(
+                        bank[:, u, block(j, P)], words[:, u : D_MODEL // 2 : 2], identity[:]
+                    )
+            nc.scalar.copy(
+                out=h_grouped[:, block(pair, PAIR * K_PASS)]
+                .bitcast(F32)
+                .rearrange("p (c u) -> p c u", u=2),
+                in_=bank[:].rearrange("p u c -> p c u"),
+            )
+            nc.vector.quantize_mx(
+                out=h_words[:, block(pair, PAIR * P)].bitcast(FP8X4),
+                scales=h_scales[:, block(pair, PAIR * P)],
+                in_=h_grouped[:, block(pair, PAIR * K_PASS)],
+            )
+
+        def first_matmul(i):
+            y = ring.tile([P, N_GROUPS, K_PASS], BF16, name="y")
+            for g in range(N_GROUPS):
+                x = psum_x.tile([P, K_PASS], F32, name="x")
+                nc.tensor.matmul_mx(
+                    out=x[:],
+                    lhsT=h_words[:, block(i, P)].bitcast(FP8X4),
+                    lhsT_scale=h_scales[:, block(i, P)],
+                    rhs=w1_words[:, block(g, K_PASS)].bitcast(FP8X4),
+                    rhs_scale=w1_scales[:, block(g, K_PASS)],
+                    start=True,
+                    stop=True,
+                )
+                nc.vector.tensor_tensor(
+                    out=y[:, g, :].rearrange("q (u p e) -> q u p e", u=2, e=2),
+                    in0=x[:].rearrange("q (p u e) -> q u p e", u=2, e=2),
+                    in1=b1_all[:, block(g, K_PASS)].rearrange("q (p u e) -> q u p e", u=2, e=2),
+                    op=ALU.add,
+                )
+            return y
+
+        def transpose_a(y):
+            grouped = ring.tile([P, N_GROUPS * K_PASS], BF16, name="grouped", align_bytes=64)
+            for b in range(N_GROUPS // PAIR):
+                bank = psum_a.tile([P, 2, PAIR * P], F32, name="a_bank")
+                for j in range(PAIR):
+                    words = y[:, PAIR * b + j, :].bitcast(F32)
+                    for u in range(2):
+                        nc.tensor.transpose(
+                            bank[:, u, block(j, P)], words[:, block(u, P)], identity[:]
+                        )
+                nc.scalar.activation(
+                    out=grouped[:, block(b, PAIR * K_PASS)].rearrange(
+                        "p (c u e) -> p c u e", u=2, e=2
+                    ),
+                    in_=bank[:].bitcast(BF16).rearrange("p u (c e) -> p c u e", e=2),
+                    func=ACT.Relu,
+                )
+            return grouped
+
+        def quantise_a(grouped):
+            a_words = ring.tile([P, N_GROUPS * P], U32, name="a_words", align_bytes=64)
+            a_scales = ring.tile([P, N_GROUPS * P], U8, name="a_scales", align_bytes=64)
+            for b in range(N_GROUPS // PAIR):
+                nc.vector.quantize_mx(
+                    out=a_words[:, block(b, PAIR * P)].bitcast(FP8X4),
+                    scales=a_scales[:, block(b, PAIR * P)],
+                    in_=grouped[:, block(b, PAIR * K_PASS)],
+                )
+            return a_words, a_scales
+
+        def second_matmul(a_words, a_scales):
+            ff = psum_o.tile([P, D_MODEL], F32, name="ff")
+            for g in range(N_GROUPS):
+                nc.tensor.matmul_mx(
+                    out=ff[:],
+                    lhsT=a_words[:, block(g, P)].bitcast(FP8X4),
+                    lhsT_scale=a_scales[:, block(g, P)],
+                    rhs=w2_words[:, g, :].bitcast(FP8X4),
+                    rhs_scale=w2_scales[:, g, :],
+                    start=(g == 0),
+                    stop=(g == N_GROUPS - 1),
+                )
+            return ff
+
+        def add_residual(i, ff):
+            nc.vector.scalar_tensor_tensor(
+                out=t_sb[:, i, :],
+                in0=ff[:],
+                scalar=1.0,
+                in1=h_plus_b2[:, i, :],
+                op0=ALU.mult,
+                op1=ALU.add,
+                accum_out=t_sum[:, i : i + 1],
+            )
+            nc.scalar.activation(
+                out=squares[:], in_=t_sb[:, i, :], func=ACT.Square, accum_out=t_sq[:, i : i + 1]
+            )
+
+        y_of = {}
+        grouped_of = {}
+        quantised_of = {}
+        ff_of = {}
+        quantise_h(0)
+        for step in range(N_TILES + 3):
+            if step >= 3:
+                add_residual(step - 3, ff_of[step - 3])
+            if 2 <= step < N_TILES + 2:
+                quantised_of[step - 2] = quantise_a(grouped_of[step - 2])
+            if step < N_TILES:
+                y_of[step] = first_matmul(step)
+            if step + 1 < N_PAIRS:
+                quantise_h(step + 1)
+            if 1 <= step < N_TILES + 1:
+                grouped_of[step - 1] = transpose_a(y_of[step - 1])
+            if 2 <= step < N_TILES + 2:
+                a_words, a_scales = quantised_of[step - 2]
+                ff_of[step - 2] = second_matmul(a_words, a_scales)
+
+        totals = psum_h.tile([P, 2, N_TILES], F32, name="totals", tag="psum_h")
+        nc.tensor.matmul(out=totals[:, 0, :], lhsT=mean_weights[:], rhs=t_sum[:], start=True, stop=True)
+        nc.tensor.matmul(out=totals[:, 1, :], lhsT=mean_weights[:], rhs=t_sq[:], start=True, stop=True)
+        nc.vector.tensor_reduce(
+            out=moments[:], in_=totals[:], axis=mybir.AxisListType.X, op=ALU.add
+        )
+        mean = moments[:, 0:1]
+        mean_of_squares = moments[:, 1:2]
+        nc.vector.scalar_tensor_tensor(
+            out=minus_var[:],
+            in0=mean,
+            scalar=mean,
+            in1=mean_of_squares,
+            op0=ALU.mult,
+            op1=ALU.subtract,
+        )
+        nc.scalar.activation(out=std[:], in_=minus_var[:], func=ACT.Sqrt, scale=-1.0, bias=eps[:])
+        nc.vector.reciprocal(out=rstd[:], in_=std[:])
+        nc.vector.tensor_scalar(
+            out=shift[:], in0=mean, scalar1=rstd[:], scalar2=-1.0, op0=ALU.mult, op1=ALU.mult
+        )
+        for i in range(N_TILES):
+            if i % 2 == 0:
+                nc.vector.tensor_scalar(
+                    out=t_sb[:, i, :],
+                    in0=t_sb[:, i, :],
+                    scalar1=rstd[:],
+                    scalar2=shift[:],
+                    op0=ALU.mult,
+                    op1=ALU.add,
+                )
+            else:
+                nc.scalar.activation(
+                    out=t_sb[:, i, :],
+                    in_=t_sb[:, i, :],
+                    func=ACT.Identity,
+                    scale=rstd[:],
+                    bias=shift[:],
+                )
+            nc.sync.dma_start(out=out_rows[:, i, :], in_=t_sb[:, i, :])

@@ -13,16 +13,23 @@ ALU = mybir.AluOpType
 ACT = mybir.ActivationFunctionType
 
 P = 128
-K_PASS = 4 * P
+PACK = 4
+K_PASS = PACK * P
 TOKENS = 1024
 D_MODEL = 512
 D_FF = 2048
 EPS = 1e-5
 N_TILES = TOKENS // P
-N_GROUPS = D_FF // K_PASS
+N_HALVES = 2
+HALF = TOKENS // N_HALVES
+HALF_TILES = HALF // P
 PAIR = 2
-N_PAIRS = N_TILES // PAIR
-QUADRANTS = 4
+HALF_PAIRS = HALF_TILES // PAIR
+N_GROUPS = D_FF // K_PASS
+QUADS = K_PASS // P
+N_BLOCKS = D_FF // P
+N_SLOTS = N_HALVES * N_GROUPS
+VECTOR_QUAD = 0
 
 FLOPS = 2 * TOKENS * D_MODEL * D_FF * 2
 
@@ -40,14 +47,15 @@ def tile_decoderblock_pb_kernel(
 
     with ExitStack() as ctx:
         keep = ctx.enter_context(tc.tile_pool(name="keep", bufs=1))
-        ring = ctx.enter_context(tc.tile_pool(name="ring", bufs=2))
+        ring3 = ctx.enter_context(tc.tile_pool(name="ring3", bufs=3))
+        ring2 = ctx.enter_context(tc.tile_pool(name="ring2", bufs=2))
         psum_x = ctx.enter_context(tc.psum_pool(name="psum_x", bufs=4))
-        psum_a = ctx.enter_context(tc.psum_pool(name="psum_a", bufs=2))
-        psum_h = ctx.enter_context(tc.psum_pool(name="psum_h", bufs=1))
-        psum_o = ctx.enter_context(tc.psum_pool(name="psum_o", bufs=1))
+        psum_s = ctx.enter_context(tc.psum_pool(name="psum_s", bufs=4))
         ctx.enter_context(tc.manual_schedule())
 
         identity = keep.tile([P, P], F32)
+        identity_bf = keep.tile([P, P], BF16)
+        ones_bf = keep.tile([P, P], BF16)
         mean_weights = keep.tile([P, P], F32)
         eps = keep.tile([P, 1], F32)
         table_warmer = keep.tile([P, 1], F32)
@@ -59,8 +67,9 @@ def tile_decoderblock_pb_kernel(
         w1_scales = keep.tile([P, D_FF], U8, align_bytes=64)
         w2_words = keep.tile([P, N_GROUPS, D_MODEL], U32, align_bytes=64)
         w2_scales = keep.tile([P, N_GROUPS, D_MODEL], U8, align_bytes=64)
-        b1_all = keep.tile([P, D_FF], BF16)
-        b2_all = keep.tile([P, D_MODEL], BF16)
+        b1_rows = keep.tile([P, P], BF16)
+        b1_cols = keep.tile([P, N_BLOCKS], F32)
+        b2_rows = keep.tile([P, D_MODEL], BF16)
         h_plus_b2 = keep.tile([P, N_TILES, D_MODEL], F32)
         t_sb = keep.tile([P, N_TILES, D_MODEL], F32)
         squares = keep.tile([P, D_MODEL], BF16)
@@ -72,17 +81,27 @@ def tile_decoderblock_pb_kernel(
         rstd = keep.tile([P, 1], F32)
         shift = keep.tile([P, 1], F32)
 
+        nc.vector.memset(b1_rows[:].bitcast(I32), 0)
         nc.vector.memset(w1_scales[:].bitcast(I32), 0)
+        nc.vector.memset(b2_rows[:].bitcast(I32), 0)
         nc.vector.memset(w2_scales[:].bitcast(I32), 0)
+        nc.vector.memset(ones_bf[:], 1.0)
         nc.vector.memset(eps[:], EPS)
         nc.vector.memset(mean_weights[:], 1.0 / (TOKENS * D_MODEL))
+        make_identity(nc, identity[:])
+        make_identity(nc, identity_bf[:])
+        nc.scalar.activation(out=table_warmer[:], in_=eps[:], func=ACT.Sqrt)
 
         def load_h(pair):
             tiles = block(pair, PAIR)
             nc.sync.dma_start(out=h_sb[:, tiles, :], in_=h_rows[:, tiles, :])
 
         load_h(0)
-        for quad in range(QUADRANTS):
+        load_h(1)
+        nc.sync.dma_start(
+            out=b1_rows[0:N_BLOCKS, :], in_=b_ff1.rearrange("(j c) -> j c", c=P)
+        )
+        for quad in range(QUADS):
             nc.sync.dma_start(
                 out=w1_scales[32 * quad : 32 * quad + 4, :].bitcast(I32),
                 in_=w_ff1_scales[0, 4 * quad : 4 * quad + 4, :].bitcast(I32),
@@ -92,9 +111,10 @@ def tile_decoderblock_pb_kernel(
             nc.sync.dma_start(
                 out=w1_words[:, block(g, K_PASS)].bitcast(I32), in_=w1_dram[:, block(g, K_PASS)]
             )
-        load_h(1)
+        nc.sync.dma_start(out=b2_rows[0:1, :], in_=b_ff2.rearrange("(o n) -> o n", o=1))
         load_h(2)
-        for quad in range(QUADRANTS):
+        load_h(3)
+        for quad in range(QUADS):
             nc.sync.dma_start(
                 out=w2_scales[32 * quad : 32 * quad + 4, :, :].bitcast(I32),
                 in_=w_ff2_scales[:, 4 * quad : 4 * quad + 4, :]
@@ -106,27 +126,17 @@ def tile_decoderblock_pb_kernel(
                 out=w2_words[:, g, :].bitcast(I32),
                 in_=w_ff2_words[g].rearrange("p n t -> p (n t)").bitcast(I32),
             )
-        load_h(3)
-
-        nc.gpsimd.dma_start(out=b1_all[:], in_=b_ff1.partition_broadcast(P))
-        make_identity(nc, identity[:])
-        nc.gpsimd.dma_start(out=b2_all[:], in_=b_ff2.partition_broadcast(P))
-        for i in range(N_TILES):
-            nc.gpsimd.tensor_tensor(
-                out=h_plus_b2[:, i, :], in0=h_sb[:, i, :], in1=b2_all[:], op=ALU.add
-            )
-
-        nc.scalar.activation(out=table_warmer[:], in_=eps[:], func=ACT.Sqrt)
 
         def quantise_h(pair):
-            bank = psum_h.tile([P, 2, PAIR * P], F32, name="h_bank", tag="psum_h")
+            bank = psum_s.tile([P, 2, PAIR * P], F32, name="h_bank", tag="shared")
             for j in range(PAIR):
                 words = h_sb[:, PAIR * pair + j, :].bitcast(F32)
                 for u in range(2):
                     nc.tensor.transpose(
                         bank[:, u, block(j, P)], words[:, u : D_MODEL // 2 : 2], identity[:]
                     )
-            nc.scalar.copy(
+            copy = nc.scalar.copy if pair % 2 == 0 else nc.vector.tensor_copy
+            copy(
                 out=h_grouped[:, block(pair, PAIR * K_PASS)]
                 .bitcast(F32)
                 .rearrange("p (c u) -> p c u", u=2),
@@ -138,106 +148,122 @@ def tile_decoderblock_pb_kernel(
                 in_=h_grouped[:, block(pair, PAIR * K_PASS)],
             )
 
-        def first_matmul(i):
-            y = ring.tile([P, N_GROUPS, K_PASS], BF16, name="y")
-            for g in range(N_GROUPS):
-                x = psum_x.tile([P, K_PASS], F32, name="x")
+        def first_matmul(slot):
+            half, g = divmod(slot, N_GROUPS)
+            a_rows = ring3.tile([P, QUADS, HALF], BF16, name="a_rows")
+            a_planes = ring3.tile([P, PACK, HALF], BF16, name="a_planes")
+            for quad in range(QUADS):
+                j = QUADS * g + quad
+                x = psum_x.tile([P, HALF], F32, name="x")
                 nc.tensor.matmul_mx(
                     out=x[:],
-                    lhsT=h_words[:, block(i, P)].bitcast(FP8X4),
-                    lhsT_scale=h_scales[:, block(i, P)],
-                    rhs=w1_words[:, block(g, K_PASS)].bitcast(FP8X4),
-                    rhs_scale=w1_scales[:, block(g, K_PASS)],
+                    lhsT=w1_words[:, block(j, P)].bitcast(FP8X4),
+                    lhsT_scale=w1_scales[:, block(j, P)],
+                    rhs=h_words[:, block(half, HALF)].bitcast(FP8X4),
+                    rhs_scale=h_scales[:, block(half, HALF)],
                     start=True,
                     stop=True,
                 )
-                nc.vector.tensor_tensor(
-                    out=y[:, g, :].rearrange("q (u p e) -> q u p e", u=2, e=2),
-                    in0=x[:].rearrange("q (p u e) -> q u p e", u=2, e=2),
-                    in1=b1_all[:, block(g, K_PASS)].rearrange("q (p u e) -> q u p e", u=2, e=2),
-                    op=ALU.add,
+                if quad == VECTOR_QUAD:
+                    nc.vector.tensor_scalar(
+                        out=a_rows[:, quad, :],
+                        in0=x[:],
+                        scalar1=b1_cols[:, j : j + 1],
+                        scalar2=0.0,
+                        op0=ALU.add,
+                        op1=ALU.max,
+                    )
+                else:
+                    nc.scalar.activation(
+                        out=a_rows[:, quad, :], in_=x[:], func=ACT.Relu, bias=b1_cols[:, j : j + 1]
+                    )
+                nc.sync.dma_start(
+                    out=a_planes[32 * quad : 32 * quad + 32, :, :], in_=a_rows[:, quad, :]
                 )
-            return y
+            return a_planes
 
-        def transpose_a(y):
-            grouped = ring.tile([P, N_GROUPS * K_PASS], BF16, name="grouped", align_bytes=64)
-            for b in range(N_GROUPS // PAIR):
-                bank = psum_a.tile([P, 2, PAIR * P], F32, name="a_bank")
-                for j in range(PAIR):
-                    words = y[:, PAIR * b + j, :].bitcast(F32)
-                    for u in range(2):
-                        nc.tensor.transpose(
-                            bank[:, u, block(j, P)], words[:, block(u, P)], identity[:]
-                        )
-                nc.scalar.activation(
-                    out=grouped[:, block(b, PAIR * K_PASS)].rearrange(
-                        "p (c u e) -> p c u e", u=2, e=2
-                    ),
-                    in_=bank[:].bitcast(BF16).rearrange("p u (c e) -> p c u e", e=2),
-                    func=ACT.Relu,
-                )
-            return grouped
-
-        def quantise_a(grouped):
-            a_words = ring.tile([P, N_GROUPS * P], U32, name="a_words", align_bytes=64)
-            a_scales = ring.tile([P, N_GROUPS * P], U8, name="a_scales", align_bytes=64)
-            for b in range(N_GROUPS // PAIR):
-                nc.vector.quantize_mx(
-                    out=a_words[:, block(b, PAIR * P)].bitcast(FP8X4),
-                    scales=a_scales[:, block(b, PAIR * P)],
-                    in_=grouped[:, block(b, PAIR * K_PASS)],
-                )
+        def quantise_a(a_planes):
+            grouped = ring2.tile([P, PACK * HALF], BF16, name="grouped", align_bytes=64)
+            a_words = ring2.tile([P, HALF], U32, name="a_words", align_bytes=64)
+            a_scales = ring2.tile([P, HALF], U8, name="a_scales", align_bytes=64)
+            nc.vector.tensor_copy(
+                out=grouped[:].rearrange("p (c i t) -> p c t i", i=4, t=PACK),
+                in_=a_planes[:].rearrange("p t (c i) -> p c t i", i=4),
+            )
+            nc.vector.quantize_mx(
+                out=a_words[:].bitcast(FP8X4), scales=a_scales[:], in_=grouped[:]
+            )
             return a_words, a_scales
 
-        def second_matmul(a_words, a_scales):
-            ff = psum_o.tile([P, D_MODEL], F32, name="ff")
-            for g in range(N_GROUPS):
+        def second_matmul(g, a_words, a_scales, sums):
+            for k in range(HALF_TILES):
                 nc.tensor.matmul_mx(
-                    out=ff[:],
-                    lhsT=a_words[:, block(g, P)].bitcast(FP8X4),
-                    lhsT_scale=a_scales[:, block(g, P)],
+                    out=sums[k][:],
+                    lhsT=a_words[:, block(k, P)].bitcast(FP8X4),
+                    lhsT_scale=a_scales[:, block(k, P)],
                     rhs=w2_words[:, g, :].bitcast(FP8X4),
                     rhs_scale=w2_scales[:, g, :],
                     start=(g == 0),
                     stop=(g == N_GROUPS - 1),
                 )
-            return ff
 
-        def add_residual(i, ff):
-            nc.vector.scalar_tensor_tensor(
-                out=t_sb[:, i, :],
-                in0=ff[:],
-                scalar=1.0,
-                in1=h_plus_b2[:, i, :],
-                op0=ALU.mult,
-                op1=ALU.add,
-                accum_out=t_sum[:, i : i + 1],
-            )
-            nc.scalar.activation(
-                out=squares[:], in_=t_sb[:, i, :], func=ACT.Square, accum_out=t_sq[:, i : i + 1]
-            )
+        def add_residual(half, sums):
+            for k in range(HALF_TILES):
+                i = HALF_TILES * half + k
+                nc.vector.scalar_tensor_tensor(
+                    out=t_sb[:, i, :],
+                    in0=sums[k][:],
+                    scalar=1.0,
+                    in1=h_plus_b2[:, i, :],
+                    op0=ALU.mult,
+                    op1=ALU.add,
+                    accum_out=t_sum[:, i : i + 1],
+                )
 
-        y_of = {}
-        grouped_of = {}
+        def sum_squares(half):
+            for i in range(HALF_TILES * half, HALF_TILES * (half + 1)):
+                nc.scalar.activation(
+                    out=squares[:], in_=t_sb[:, i, :], func=ACT.Square, accum_out=t_sq[:, i : i + 1]
+                )
+
+        for pair in range(HALF_PAIRS):
+            quantise_h(pair)
+        b1_bank = psum_s.tile([P, P], BF16, name="b1_bank", tag="shared")
+        nc.tensor.transpose(b1_bank[:], b1_rows[:], identity_bf[:])
+        nc.vector.tensor_copy(out=b1_cols[:], in_=b1_bank[:, 0:N_BLOCKS])
+        b2_bank = psum_s.tile([P, D_MODEL], F32, name="b2_bank", tag="shared")
+        nc.tensor.matmul(out=b2_bank[:], lhsT=ones_bf[:], rhs=b2_rows[:], start=True, stop=True)
+
+        planes_of = {}
         quantised_of = {}
-        ff_of = {}
-        quantise_h(0)
-        for step in range(N_TILES + 3):
-            if step >= 3:
-                add_residual(step - 3, ff_of[step - 3])
-            if 2 <= step < N_TILES + 2:
-                quantised_of[step - 2] = quantise_a(grouped_of[step - 2])
-            if step < N_TILES:
-                y_of[step] = first_matmul(step)
-            if step + 1 < N_PAIRS:
-                quantise_h(step + 1)
-            if 1 <= step < N_TILES + 1:
-                grouped_of[step - 1] = transpose_a(y_of[step - 1])
-            if 2 <= step < N_TILES + 2:
-                a_words, a_scales = quantised_of[step - 2]
-                ff_of[step - 2] = second_matmul(a_words, a_scales)
+        sums_of = {}
+        for turn in range(N_SLOTS + 4):
+            if turn < N_SLOTS:
+                planes_of[turn] = first_matmul(turn)
+            if turn < HALF_PAIRS:
+                quantise_h(HALF_PAIRS + turn)
+            if turn < N_HALVES:
+                for i in range(HALF_TILES * turn, HALF_TILES * (turn + 1)):
+                    nc.vector.tensor_tensor(
+                        out=h_plus_b2[:, i, :], in0=b2_bank[:], in1=h_sb[:, i, :], op=ALU.add
+                    )
+            if 0 <= turn - 3 < N_SLOTS:
+                half, g = divmod(turn - 3, N_GROUPS)
+                if g == 0:
+                    sums_of[half] = [
+                        psum_s.tile([P, D_MODEL], F32, name="ff%d" % k, tag="shared")
+                        for k in range(HALF_TILES)
+                    ]
+                a_words, a_scales = quantised_of[turn - 3]
+                second_matmul(g, a_words, a_scales, sums_of[half])
+            if 0 <= turn - 2 < N_SLOTS:
+                quantised_of[turn - 2] = quantise_a(planes_of[turn - 2])
+            if 0 <= turn - 3 < N_SLOTS and (turn - 3) % N_GROUPS == N_GROUPS - 1:
+                add_residual((turn - 3) // N_GROUPS, sums_of[(turn - 3) // N_GROUPS])
+            if 0 <= turn - 4 < N_SLOTS and (turn - 4) % N_GROUPS == N_GROUPS - 1:
+                sum_squares((turn - 4) // N_GROUPS)
 
-        totals = psum_h.tile([P, 2, N_TILES], F32, name="totals", tag="psum_h")
+        totals = psum_s.tile([P, 2, N_TILES], F32, name="totals", tag="shared")
         nc.tensor.matmul(out=totals[:, 0, :], lhsT=mean_weights[:], rhs=t_sum[:], start=True, stop=True)
         nc.tensor.matmul(out=totals[:, 1, :], lhsT=mean_weights[:], rhs=t_sq[:], start=True, stop=True)
         nc.vector.tensor_reduce(

@@ -29,7 +29,7 @@ N_GROUPS = D_FF // K_PASS
 QUADS = K_PASS // P
 N_BLOCKS = D_FF // P
 N_SLOTS = N_HALVES * N_GROUPS
-VECTOR_QUAD = 0
+FILL_TURNS = 2
 
 FLOPS = 2 * TOKENS * D_MODEL * D_FF * 2
 
@@ -47,7 +47,7 @@ def tile_decoderblock_pb_kernel(
 
     with ExitStack() as ctx:
         keep = ctx.enter_context(tc.tile_pool(name="keep", bufs=1))
-        ring3 = ctx.enter_context(tc.tile_pool(name="ring3", bufs=3))
+        ring4 = ctx.enter_context(tc.tile_pool(name="ring4", bufs=4))
         ring2 = ctx.enter_context(tc.tile_pool(name="ring2", bufs=2))
         psum_x = ctx.enter_context(tc.psum_pool(name="psum_x", bufs=4))
         psum_s = ctx.enter_context(tc.psum_pool(name="psum_s", bufs=4))
@@ -70,6 +70,7 @@ def tile_decoderblock_pb_kernel(
         b1_rows = keep.tile([P, P], BF16)
         b1_cols = keep.tile([P, N_BLOCKS], F32)
         b2_rows = keep.tile([P, D_MODEL], BF16)
+        b2_all = keep.tile([P, D_MODEL], BF16)
         h_plus_b2 = keep.tile([P, N_TILES, D_MODEL], F32)
         t_sb = keep.tile([P, N_TILES, D_MODEL], F32)
         squares = keep.tile([P, D_MODEL], BF16)
@@ -79,7 +80,6 @@ def tile_decoderblock_pb_kernel(
         minus_var = keep.tile([P, 1], F32)
         std = keep.tile([P, 1], F32)
         rstd = keep.tile([P, 1], F32)
-        shift = keep.tile([P, 1], F32)
 
         nc.vector.memset(b1_rows[:].bitcast(I32), 0)
         nc.vector.memset(w1_scales[:].bitcast(I32), 0)
@@ -150,8 +150,8 @@ def tile_decoderblock_pb_kernel(
 
         def first_matmul(slot):
             half, g = divmod(slot, N_GROUPS)
-            a_rows = ring3.tile([P, QUADS, HALF], BF16, name="a_rows")
-            a_planes = ring3.tile([P, PACK, HALF], BF16, name="a_planes")
+            a_rows = ring4.tile([P, QUADS, HALF], BF16, name="a_rows")
+            a_planes = ring4.tile([P, PACK, HALF], BF16, name="a_planes")
             for quad in range(QUADS):
                 j = QUADS * g + quad
                 x = psum_x.tile([P, HALF], F32, name="x")
@@ -164,7 +164,7 @@ def tile_decoderblock_pb_kernel(
                     start=True,
                     stop=True,
                 )
-                if quad == VECTOR_QUAD:
+                if slot < FILL_TURNS and quad % 2 == 1:
                     nc.vector.tensor_scalar(
                         out=a_rows[:, quad, :],
                         in0=x[:],
@@ -182,14 +182,17 @@ def tile_decoderblock_pb_kernel(
                 )
             return a_planes
 
-        def quantise_a(a_planes):
+        def regroup_a(a_planes):
             grouped = ring2.tile([P, PACK * HALF], BF16, name="grouped", align_bytes=64)
-            a_words = ring2.tile([P, HALF], U32, name="a_words", align_bytes=64)
-            a_scales = ring2.tile([P, HALF], U8, name="a_scales", align_bytes=64)
             nc.vector.tensor_copy(
                 out=grouped[:].rearrange("p (c i t) -> p c t i", i=4, t=PACK),
                 in_=a_planes[:].rearrange("p t (c i) -> p c t i", i=4),
             )
+            return grouped
+
+        def quantise_a(grouped):
+            a_words = ring2.tile([P, HALF], U32, name="a_words", align_bytes=64)
+            a_scales = ring2.tile([P, HALF], U8, name="a_scales", align_bytes=64)
             nc.vector.quantize_mx(
                 out=a_words[:].bitcast(FP8X4), scales=a_scales[:], in_=grouped[:]
             )
@@ -233,35 +236,41 @@ def tile_decoderblock_pb_kernel(
         nc.vector.tensor_copy(out=b1_cols[:], in_=b1_bank[:, 0:N_BLOCKS])
         b2_bank = psum_s.tile([P, D_MODEL], F32, name="b2_bank", tag="shared")
         nc.tensor.matmul(out=b2_bank[:], lhsT=ones_bf[:], rhs=b2_rows[:], start=True, stop=True)
+        nc.scalar.copy(out=b2_all[:], in_=b2_bank[:])
+        for i in range(N_TILES):
+            nc.gpsimd.tensor_tensor(
+                out=h_plus_b2[:, i, :], in0=h_sb[:, i, :], in1=b2_all[:], op=ALU.add
+            )
+
+        def closes_half(slot):
+            return 0 <= slot < N_SLOTS and slot % N_GROUPS == N_GROUPS - 1
 
         planes_of = {}
+        grouped_of = {}
         quantised_of = {}
         sums_of = {}
-        for turn in range(N_SLOTS + 4):
+        for turn in range(N_SLOTS + 5):
             if turn < N_SLOTS:
                 planes_of[turn] = first_matmul(turn)
             if turn < HALF_PAIRS:
                 quantise_h(HALF_PAIRS + turn)
-            if turn < N_HALVES:
-                for i in range(HALF_TILES * turn, HALF_TILES * (turn + 1)):
-                    nc.vector.tensor_tensor(
-                        out=h_plus_b2[:, i, :], in0=b2_bank[:], in1=h_sb[:, i, :], op=ALU.add
-                    )
-            if 0 <= turn - 3 < N_SLOTS:
-                half, g = divmod(turn - 3, N_GROUPS)
+            if 0 <= turn - 4 < N_SLOTS:
+                half, g = divmod(turn - 4, N_GROUPS)
                 if g == 0:
                     sums_of[half] = [
                         psum_s.tile([P, D_MODEL], F32, name="ff%d" % k, tag="shared")
                         for k in range(HALF_TILES)
                     ]
-                a_words, a_scales = quantised_of[turn - 3]
+                a_words, a_scales = quantised_of[turn - 4]
                 second_matmul(g, a_words, a_scales, sums_of[half])
             if 0 <= turn - 2 < N_SLOTS:
-                quantised_of[turn - 2] = quantise_a(planes_of[turn - 2])
-            if 0 <= turn - 3 < N_SLOTS and (turn - 3) % N_GROUPS == N_GROUPS - 1:
-                add_residual((turn - 3) // N_GROUPS, sums_of[(turn - 3) // N_GROUPS])
-            if 0 <= turn - 4 < N_SLOTS and (turn - 4) % N_GROUPS == N_GROUPS - 1:
-                sum_squares((turn - 4) // N_GROUPS)
+                grouped_of[turn - 2] = regroup_a(planes_of[turn - 2])
+            if 0 <= turn - 3 < N_SLOTS:
+                quantised_of[turn - 3] = quantise_a(grouped_of[turn - 3])
+            if closes_half(turn - 4):
+                add_residual((turn - 4) // N_GROUPS, sums_of[(turn - 4) // N_GROUPS])
+            if closes_half(turn - 5):
+                sum_squares((turn - 5) // N_GROUPS)
 
         totals = psum_s.tile([P, 2, N_TILES], F32, name="totals", tag="shared")
         nc.tensor.matmul(out=totals[:, 0, :], lhsT=mean_weights[:], rhs=t_sum[:], start=True, stop=True)
@@ -281,25 +290,13 @@ def tile_decoderblock_pb_kernel(
         )
         nc.scalar.activation(out=std[:], in_=minus_var[:], func=ACT.Sqrt, scale=-1.0, bias=eps[:])
         nc.vector.reciprocal(out=rstd[:], in_=std[:])
-        nc.vector.tensor_scalar(
-            out=shift[:], in0=mean, scalar1=rstd[:], scalar2=-1.0, op0=ALU.mult, op1=ALU.mult
-        )
         for i in range(N_TILES):
-            if i % 2 == 0:
-                nc.vector.tensor_scalar(
-                    out=t_sb[:, i, :],
-                    in0=t_sb[:, i, :],
-                    scalar1=rstd[:],
-                    scalar2=shift[:],
-                    op0=ALU.mult,
-                    op1=ALU.add,
-                )
-            else:
-                nc.scalar.activation(
-                    out=t_sb[:, i, :],
-                    in_=t_sb[:, i, :],
-                    func=ACT.Identity,
-                    scale=rstd[:],
-                    bias=shift[:],
-                )
+            nc.vector.tensor_scalar(
+                out=t_sb[:, i, :],
+                in0=t_sb[:, i, :],
+                scalar1=mean,
+                scalar2=rstd[:],
+                op0=ALU.subtract,
+                op1=ALU.mult,
+            )
             nc.sync.dma_start(out=out_rows[:, i, :], in_=t_sb[:, i, :])

@@ -27,6 +27,8 @@ PAIR = 2
 HALF_PAIRS = HALF_TILES // PAIR
 N_GROUPS = D_FF // K_PASS
 QUADS = K_PASS // P
+AS_GIVEN = "p (i v r) -> p v i r"
+SORTED = "p (v i r) -> p v i r"
 N_BLOCKS = D_FF // P
 N_SLOTS = N_HALVES * N_GROUPS
 FILL_TURNS = 2
@@ -63,11 +65,14 @@ def tile_decoderblock_pb_kernel(
         h_grouped = keep.tile([P, N_TILES * K_PASS], BF16, align_bytes=64)
         h_words = keep.tile([P, TOKENS], U32, align_bytes=64)
         h_scales = keep.tile([P, TOKENS], U8, align_bytes=64)
+        w1_words_given = keep.tile([P, D_FF], U32)
+        w1_scales_given = keep.tile([P, D_FF], U8)
         w1_words = keep.tile([P, D_FF], U32, align_bytes=64)
         w1_scales = keep.tile([P, D_FF], U8, align_bytes=64)
         w2_words = keep.tile([P, N_GROUPS, D_MODEL], U32, align_bytes=64)
         w2_scales = keep.tile([P, N_GROUPS, D_MODEL], U8, align_bytes=64)
-        b1_rows = keep.tile([P, P], BF16)
+        b1_given = keep.tile([P, K_PASS], BF16)
+        b1_sorted = keep.tile([P, K_PASS], BF16)
         b1_cols = keep.tile([P, N_BLOCKS], F32)
         b2_rows = keep.tile([P, D_MODEL], BF16)
         b2_all = keep.tile([P, D_MODEL], BF16)
@@ -81,8 +86,8 @@ def tile_decoderblock_pb_kernel(
         std = keep.tile([P, 1], F32)
         rstd = keep.tile([P, 1], F32)
 
-        nc.vector.memset(b1_rows[:].bitcast(I32), 0)
-        nc.vector.memset(w1_scales[:].bitcast(I32), 0)
+        nc.vector.memset(b1_given[:].bitcast(I32), 0)
+        nc.vector.memset(w1_scales_given[:].bitcast(I32), 0)
         nc.vector.memset(b2_rows[:].bitcast(I32), 0)
         nc.vector.memset(w2_scales[:].bitcast(I32), 0)
         nc.vector.memset(ones_bf[:], 1.0)
@@ -99,17 +104,18 @@ def tile_decoderblock_pb_kernel(
         load_h(0)
         load_h(1)
         nc.sync.dma_start(
-            out=b1_rows[0:N_BLOCKS, :], in_=b_ff1.rearrange("(j c) -> j c", c=P)
+            out=b1_given[0:N_GROUPS, :], in_=b_ff1.rearrange("(g f) -> g f", f=K_PASS)
         )
         for quad in range(QUADS):
             nc.sync.dma_start(
-                out=w1_scales[32 * quad : 32 * quad + 4, :].bitcast(I32),
+                out=w1_scales_given[32 * quad : 32 * quad + 4, :].bitcast(I32),
                 in_=w_ff1_scales[0, 4 * quad : 4 * quad + 4, :].bitcast(I32),
             )
         w1_dram = w_ff1_words[0].rearrange("p n t -> p (n t)").bitcast(I32)
         for g in range(N_GROUPS):
             nc.sync.dma_start(
-                out=w1_words[:, block(g, K_PASS)].bitcast(I32), in_=w1_dram[:, block(g, K_PASS)]
+                out=w1_words_given[:, block(g, K_PASS)].bitcast(I32),
+                in_=w1_dram[:, block(g, K_PASS)],
             )
         nc.sync.dma_start(out=b2_rows[0:1, :], in_=b_ff2.rearrange("(o n) -> o n", o=1))
         load_h(2)
@@ -148,6 +154,14 @@ def tile_decoderblock_pb_kernel(
                 in_=h_grouped[:, block(pair, PAIR * K_PASS)],
             )
 
+        def sort_w1_words(g):
+            nc.vector.tensor_copy(
+                out=w1_words[:, block(g, K_PASS)].bitcast(I32).rearrange(SORTED, v=QUADS, r=PACK),
+                in_=w1_words_given[:, block(g, K_PASS)]
+                .bitcast(I32)
+                .rearrange(AS_GIVEN, v=QUADS, r=PACK),
+            )
+
         def first_matmul(slot):
             half, g = divmod(slot, N_GROUPS)
             a_rows = ring4.tile([P, QUADS, HALF], BF16, name="a_rows")
@@ -177,9 +191,7 @@ def tile_decoderblock_pb_kernel(
                     nc.scalar.activation(
                         out=a_rows[:, quad, :], in_=x[:], func=ACT.Relu, bias=b1_cols[:, j : j + 1]
                     )
-                nc.sync.dma_start(
-                    out=a_planes[32 * quad : 32 * quad + 32, :, :], in_=a_rows[:, quad, :]
-                )
+                nc.sync.dma_start(out=a_planes[quad:P:QUADS, :, :], in_=a_rows[:, quad, :])
             return a_planes
 
         def regroup_a(a_planes):
@@ -229,11 +241,25 @@ def tile_decoderblock_pb_kernel(
                     out=squares[:], in_=t_sb[:, i, :], func=ACT.Square, accum_out=t_sq[:, i : i + 1]
                 )
 
+        nc.vector.tensor_copy(
+            out=b1_sorted[:].rearrange(SORTED, v=QUADS, r=PACK),
+            in_=b1_given[:].rearrange(AS_GIVEN, v=QUADS, r=PACK),
+        )
+        nc.vector.tensor_copy(
+            out=w1_scales[:].bitcast(I32).rearrange("p (g v i) -> p g v i", g=N_GROUPS, v=QUADS),
+            in_=w1_scales_given[:]
+            .bitcast(I32)
+            .rearrange("p (g i v) -> p g v i", g=N_GROUPS, v=QUADS),
+        )
         for pair in range(HALF_PAIRS):
             quantise_h(pair)
-        b1_bank = psum_s.tile([P, P], BF16, name="b1_bank", tag="shared")
-        nc.tensor.transpose(b1_bank[:], b1_rows[:], identity_bf[:])
-        nc.vector.tensor_copy(out=b1_cols[:], in_=b1_bank[:, 0:N_BLOCKS])
+        sort_w1_words(0)
+        b1_bank = psum_s.tile([P, QUADS, P], BF16, name="b1_bank", tag="shared")
+        for v in range(QUADS):
+            nc.tensor.transpose(b1_bank[:, v, :], b1_sorted[:, block(v, P)], identity_bf[:])
+        nc.vector.tensor_copy(
+            out=b1_cols[:].rearrange("p (g v) -> p v g", v=QUADS), in_=b1_bank[:, :, 0:N_GROUPS]
+        )
         b2_bank = psum_s.tile([P, D_MODEL], F32, name="b2_bank", tag="shared")
         nc.tensor.matmul(out=b2_bank[:], lhsT=ones_bf[:], rhs=b2_rows[:], start=True, stop=True)
         nc.scalar.copy(out=b2_all[:], in_=b2_bank[:])
@@ -252,6 +278,8 @@ def tile_decoderblock_pb_kernel(
         for turn in range(N_SLOTS + 5):
             if turn < N_SLOTS:
                 planes_of[turn] = first_matmul(turn)
+            if turn + 1 < N_GROUPS:
+                sort_w1_words(turn + 1)
             if turn < HALF_PAIRS:
                 quantise_h(HALF_PAIRS + turn)
             if 0 <= turn - 4 < N_SLOTS:

@@ -66,11 +66,11 @@ def tile_decoderblock_pb_kernel(
         h_words = keep.tile([P, TOKENS], U32, align_bytes=64)
         h_scales = keep.tile([P, TOKENS], U8, align_bytes=64)
         w1_words_given = keep.tile([P, D_FF], U32)
-        w1_scales_given = keep.tile([P, D_FF], U8)
+        w1_scales_given = keep.tile([P, K_PASS], U8)
         w1_words = keep.tile([P, D_FF], U32, align_bytes=64)
-        w1_scales = keep.tile([P, D_FF], U8, align_bytes=64)
+        w1_scales = keep.tile([P, K_PASS], U8, align_bytes=64)
         w2_words = keep.tile([P, N_GROUPS, D_MODEL], U32, align_bytes=64)
-        w2_scales = keep.tile([P, N_GROUPS, D_MODEL], U8, align_bytes=64)
+        w2_scales = keep.tile([P, D_MODEL], U8, align_bytes=64)
         b1_given = keep.tile([P, K_PASS], BF16)
         b1_sorted = keep.tile([P, K_PASS], BF16)
         b1_cols = keep.tile([P, N_BLOCKS], F32)
@@ -79,8 +79,7 @@ def tile_decoderblock_pb_kernel(
         h_plus_b2 = keep.tile([P, N_TILES, D_MODEL], F32)
         t_sb = keep.tile([P, N_TILES, D_MODEL], F32)
         squares = keep.tile([P, D_MODEL], BF16)
-        t_sum = keep.tile([P, N_TILES], F32)
-        t_sq = keep.tile([P, N_TILES], F32)
+        t_sums = keep.tile([P, 2, N_TILES], F32)
         moments = keep.tile([P, 2], F32)
         minus_var = keep.tile([P, 1], F32)
         std = keep.tile([P, 1], F32)
@@ -108,24 +107,29 @@ def tile_decoderblock_pb_kernel(
         )
         for quad in range(QUADS):
             nc.sync.dma_start(
-                out=w1_scales_given[32 * quad : 32 * quad + 4, :].bitcast(I32),
-                in_=w_ff1_scales[0, 4 * quad : 4 * quad + 4, :].bitcast(I32),
+                out=w1_scales_given[32 * quad : 32 * quad + 16, :].bitcast(I32),
+                in_=w_ff1_scales[0, 4 * quad : 4 * quad + 4, :]
+                .bitcast(I32)
+                .rearrange("r (g n) -> g r n", g=N_GROUPS),
             )
         w1_dram = w_ff1_words[0].rearrange("p n t -> p (n t)").bitcast(I32)
-        for g in range(N_GROUPS):
+
+        def load_w1_words(g):
             nc.sync.dma_start(
                 out=w1_words_given[:, block(g, K_PASS)].bitcast(I32),
                 in_=w1_dram[:, block(g, K_PASS)],
             )
+
+        load_w1_words(0)
         nc.sync.dma_start(out=b2_rows[0:1, :], in_=b_ff2.rearrange("(o n) -> o n", o=1))
+        for g in range(1, N_GROUPS):
+            load_w1_words(g)
         load_h(2)
         load_h(3)
         for quad in range(QUADS):
             nc.sync.dma_start(
-                out=w2_scales[32 * quad : 32 * quad + 4, :, :].bitcast(I32),
-                in_=w_ff2_scales[:, 4 * quad : 4 * quad + 4, :]
-                .bitcast(I32)
-                .rearrange("g r n -> r g n"),
+                out=w2_scales[32 * quad : 32 * quad + 16, :].bitcast(I32),
+                in_=w_ff2_scales[:, 4 * quad : 4 * quad + 4, :].bitcast(I32),
             )
         for g in range(N_GROUPS):
             nc.sync.dma_start(
@@ -141,7 +145,7 @@ def tile_decoderblock_pb_kernel(
                     nc.tensor.transpose(
                         bank[:, u, block(j, P)], words[:, u : D_MODEL // 2 : 2], identity[:]
                     )
-            copy = nc.scalar.copy if pair % 2 == 0 else nc.vector.tensor_copy
+            copy = nc.scalar.copy if pair < HALF_PAIRS else nc.vector.tensor_copy
             copy(
                 out=h_grouped[:, block(pair, PAIR * K_PASS)]
                 .bitcast(F32)
@@ -172,7 +176,7 @@ def tile_decoderblock_pb_kernel(
                 nc.tensor.matmul_mx(
                     out=x[:],
                     lhsT=w1_words[:, block(j, P)].bitcast(FP8X4),
-                    lhsT_scale=w1_scales[:, block(j, P)],
+                    lhsT_scale=w1_scales[4 * g : P, block(quad, P)],
                     rhs=h_words[:, block(half, HALF)].bitcast(FP8X4),
                     rhs_scale=h_scales[:, block(half, HALF)],
                     start=True,
@@ -217,7 +221,7 @@ def tile_decoderblock_pb_kernel(
                     lhsT=a_words[:, block(k, P)].bitcast(FP8X4),
                     lhsT_scale=a_scales[:, block(k, P)],
                     rhs=w2_words[:, g, :].bitcast(FP8X4),
-                    rhs_scale=w2_scales[:, g, :],
+                    rhs_scale=w2_scales[4 * g : P, :],
                     start=(g == 0),
                     stop=(g == N_GROUPS - 1),
                 )
@@ -232,13 +236,16 @@ def tile_decoderblock_pb_kernel(
                     in1=h_plus_b2[:, i, :],
                     op0=ALU.mult,
                     op1=ALU.add,
-                    accum_out=t_sum[:, i : i + 1],
+                    accum_out=t_sums[:, 0, i : i + 1],
                 )
 
         def sum_squares(half):
             for i in range(HALF_TILES * half, HALF_TILES * (half + 1)):
                 nc.scalar.activation(
-                    out=squares[:], in_=t_sb[:, i, :], func=ACT.Square, accum_out=t_sq[:, i : i + 1]
+                    out=squares[:],
+                    in_=t_sb[:, i, :],
+                    func=ACT.Square,
+                    accum_out=t_sums[:, 1, i : i + 1],
                 )
 
         nc.vector.tensor_copy(
@@ -246,14 +253,13 @@ def tile_decoderblock_pb_kernel(
             in_=b1_given[:].rearrange(AS_GIVEN, v=QUADS, r=PACK),
         )
         nc.vector.tensor_copy(
-            out=w1_scales[:].bitcast(I32).rearrange("p (g v i) -> p g v i", g=N_GROUPS, v=QUADS),
-            in_=w1_scales_given[:]
-            .bitcast(I32)
-            .rearrange("p (g i v) -> p g v i", g=N_GROUPS, v=QUADS),
+            out=w1_scales[:].bitcast(I32).rearrange("p (v i) -> p v i", v=QUADS),
+            in_=w1_scales_given[:].bitcast(I32).rearrange("p (i v) -> p v i", v=QUADS),
         )
-        for pair in range(HALF_PAIRS):
-            quantise_h(pair)
+        quantise_h(0)
         sort_w1_words(0)
+        for pair in range(1, HALF_PAIRS):
+            quantise_h(pair)
         b1_bank = psum_s.tile([P, QUADS, P], BF16, name="b1_bank", tag="shared")
         for v in range(QUADS):
             nc.tensor.transpose(b1_bank[:, v, :], b1_sorted[:, block(v, P)], identity_bf[:])
@@ -301,8 +307,13 @@ def tile_decoderblock_pb_kernel(
                 sum_squares((turn - 5) // N_GROUPS)
 
         totals = psum_s.tile([P, 2, N_TILES], F32, name="totals", tag="shared")
-        nc.tensor.matmul(out=totals[:, 0, :], lhsT=mean_weights[:], rhs=t_sum[:], start=True, stop=True)
-        nc.tensor.matmul(out=totals[:, 1, :], lhsT=mean_weights[:], rhs=t_sq[:], start=True, stop=True)
+        nc.tensor.matmul(
+            out=totals[:].rearrange("p s i -> p (s i)"),
+            lhsT=mean_weights[:],
+            rhs=t_sums[:].rearrange("p s i -> p (s i)"),
+            start=True,
+            stop=True,
+        )
         nc.vector.tensor_reduce(
             out=moments[:], in_=totals[:], axis=mybir.AxisListType.X, op=ALU.add
         )

@@ -27,11 +27,15 @@ PAIR = 2
 HALF_PAIRS = HALF_TILES // PAIR
 N_GROUPS = D_FF // K_PASS
 QUADS = K_PASS // P
-AS_GIVEN = "p (i v r) -> p v i r"
-SORTED = "p (v i r) -> p v i r"
+AS_GIVEN = "p (m t) -> p t m"
+SORTED = "p (t m) -> p t m"
+CHUNK = 256
+HALF_CHUNKS = 2
+CHUNK_TILES = 2
 N_BLOCKS = D_FF // P
 N_SLOTS = N_HALVES * N_GROUPS
-FILL_TURNS = 2
+FILL_TURNS = 1
+SCALAR_NORM_TILES = (1, 4, 7)
 
 FLOPS = 2 * TOKENS * D_MODEL * D_FF * 2
 
@@ -49,8 +53,9 @@ def tile_decoderblock_pb_kernel(
 
     with ExitStack() as ctx:
         keep = ctx.enter_context(tc.tile_pool(name="keep", bufs=1))
+        ring3 = ctx.enter_context(tc.tile_pool(name="ring3", bufs=3))
         ring4 = ctx.enter_context(tc.tile_pool(name="ring4", bufs=4))
-        ring2 = ctx.enter_context(tc.tile_pool(name="ring2", bufs=2))
+        ring6 = ctx.enter_context(tc.tile_pool(name="ring6", bufs=6))
         psum_x = ctx.enter_context(tc.psum_pool(name="psum_x", bufs=4))
         psum_s = ctx.enter_context(tc.psum_pool(name="psum_s", bufs=4))
         ctx.enter_context(tc.manual_schedule())
@@ -84,6 +89,7 @@ def tile_decoderblock_pb_kernel(
         minus_var = keep.tile([P, 1], F32)
         std = keep.tile([P, 1], F32)
         rstd = keep.tile([P, 1], F32)
+        minus_mean_rstd = keep.tile([P, 1], F32)
 
         nc.vector.memset(b1_given[:].bitcast(I32), 0)
         nc.vector.memset(w1_scales_given[:].bitcast(I32), 0)
@@ -160,31 +166,28 @@ def tile_decoderblock_pb_kernel(
 
         def sort_w1_words(g):
             nc.vector.tensor_copy(
-                out=w1_words[:, block(g, K_PASS)].bitcast(I32).rearrange(SORTED, v=QUADS, r=PACK),
-                in_=w1_words_given[:, block(g, K_PASS)]
-                .bitcast(I32)
-                .rearrange(AS_GIVEN, v=QUADS, r=PACK),
+                out=w1_words[:, block(g, K_PASS)].bitcast(I32).rearrange(SORTED, t=PACK),
+                in_=w1_words_given[:, block(g, K_PASS)].bitcast(I32).rearrange(AS_GIVEN, t=PACK),
             )
 
         def first_matmul(slot):
             half, g = divmod(slot, N_GROUPS)
-            a_rows = ring4.tile([P, QUADS, HALF], BF16, name="a_rows")
-            a_planes = ring4.tile([P, PACK, HALF], BF16, name="a_planes")
-            for quad in range(QUADS):
-                j = QUADS * g + quad
+            a_planes = ring3.tile([P, PACK, HALF], BF16, name="a_planes")
+            for t in range(PACK):
+                j = PACK * g + t
                 x = psum_x.tile([P, HALF], F32, name="x")
                 nc.tensor.matmul_mx(
                     out=x[:],
                     lhsT=w1_words[:, block(j, P)].bitcast(FP8X4),
-                    lhsT_scale=w1_scales[4 * g : P, block(quad, P)],
+                    lhsT_scale=w1_scales[4 * g : P, block(t, P)],
                     rhs=h_words[:, block(half, HALF)].bitcast(FP8X4),
                     rhs_scale=h_scales[:, block(half, HALF)],
                     start=True,
                     stop=True,
                 )
-                if slot < FILL_TURNS and quad % 2 == 1:
+                if slot < FILL_TURNS and t % 2 == 1:
                     nc.vector.tensor_scalar(
-                        out=a_rows[:, quad, :],
+                        out=a_planes[:, t, :],
                         in0=x[:],
                         scalar1=b1_cols[:, j : j + 1],
                         scalar2=0.0,
@@ -193,33 +196,33 @@ def tile_decoderblock_pb_kernel(
                     )
                 else:
                     nc.scalar.activation(
-                        out=a_rows[:, quad, :], in_=x[:], func=ACT.Relu, bias=b1_cols[:, j : j + 1]
+                        out=a_planes[:, t, :], in_=x[:], func=ACT.Relu, bias=b1_cols[:, j : j + 1]
                     )
-                nc.sync.dma_start(out=a_planes[quad:P:QUADS, :, :], in_=a_rows[:, quad, :])
             return a_planes
 
-        def regroup_a(a_planes):
-            grouped = ring2.tile([P, PACK * HALF], BF16, name="grouped", align_bytes=64)
+        def regroup_a(a_planes, c):
+            grouped = ring4.tile([P, PACK * CHUNK], BF16, name="grouped", align_bytes=64)
             nc.vector.tensor_copy(
                 out=grouped[:].rearrange("p (c i t) -> p c t i", i=4, t=PACK),
-                in_=a_planes[:].rearrange("p t (c i) -> p c t i", i=4),
+                in_=a_planes[:, :, block(c, CHUNK)].rearrange("p t (c i) -> p c t i", i=4),
             )
             return grouped
 
         def quantise_a(grouped):
-            a_words = ring2.tile([P, HALF], U32, name="a_words", align_bytes=64)
-            a_scales = ring2.tile([P, HALF], U8, name="a_scales", align_bytes=64)
+            a_words = ring6.tile([P, CHUNK], U32, name="a_words", align_bytes=64)
+            a_scales = ring6.tile([P, CHUNK], U8, name="a_scales", align_bytes=64)
             nc.vector.quantize_mx(
                 out=a_words[:].bitcast(FP8X4), scales=a_scales[:], in_=grouped[:]
             )
             return a_words, a_scales
 
-        def second_matmul(g, a_words, a_scales, sums):
+        def second_matmul(g, quantised, sums):
             for k in range(HALF_TILES):
+                a_words, a_scales = quantised[k // CHUNK_TILES]
                 nc.tensor.matmul_mx(
                     out=sums[k][:],
-                    lhsT=a_words[:, block(k, P)].bitcast(FP8X4),
-                    lhsT_scale=a_scales[:, block(k, P)],
+                    lhsT=a_words[:, block(k % CHUNK_TILES, P)].bitcast(FP8X4),
+                    lhsT_scale=a_scales[:, block(k % CHUNK_TILES, P)],
                     rhs=w2_words[:, g, :].bitcast(FP8X4),
                     rhs_scale=w2_scales[4 * g : P, :],
                     start=(g == 0),
@@ -249,22 +252,22 @@ def tile_decoderblock_pb_kernel(
                 )
 
         nc.vector.tensor_copy(
-            out=b1_sorted[:].rearrange(SORTED, v=QUADS, r=PACK),
-            in_=b1_given[:].rearrange(AS_GIVEN, v=QUADS, r=PACK),
+            out=b1_sorted[:].rearrange(SORTED, t=PACK),
+            in_=b1_given[:].rearrange(AS_GIVEN, t=PACK),
         )
         nc.vector.tensor_copy(
-            out=w1_scales[:].bitcast(I32).rearrange("p (v i) -> p v i", v=QUADS),
-            in_=w1_scales_given[:].bitcast(I32).rearrange("p (i v) -> p v i", v=QUADS),
+            out=w1_scales[:].rearrange("p (t m) -> p m t", t=PACK),
+            in_=w1_scales_given[:].rearrange("p (m t) -> p m t", t=PACK),
         )
         quantise_h(0)
         sort_w1_words(0)
         for pair in range(1, HALF_PAIRS):
             quantise_h(pair)
-        b1_bank = psum_s.tile([P, QUADS, P], BF16, name="b1_bank", tag="shared")
-        for v in range(QUADS):
-            nc.tensor.transpose(b1_bank[:, v, :], b1_sorted[:, block(v, P)], identity_bf[:])
+        b1_bank = psum_s.tile([P, PACK, P], BF16, name="b1_bank", tag="shared")
+        for t in range(PACK):
+            nc.tensor.transpose(b1_bank[:, t, :], b1_sorted[:, block(t, P)], identity_bf[:])
         nc.vector.tensor_copy(
-            out=b1_cols[:].rearrange("p (g v) -> p v g", v=QUADS), in_=b1_bank[:, :, 0:N_GROUPS]
+            out=b1_cols[:].rearrange("p (g t) -> p t g", t=PACK), in_=b1_bank[:, :, 0:N_GROUPS]
         )
         b2_bank = psum_s.tile([P, D_MODEL], F32, name="b2_bank", tag="shared")
         nc.tensor.matmul(out=b2_bank[:], lhsT=ones_bf[:], rhs=b2_rows[:], start=True, stop=True)
@@ -278,33 +281,32 @@ def tile_decoderblock_pb_kernel(
             return 0 <= slot < N_SLOTS and slot % N_GROUPS == N_GROUPS - 1
 
         planes_of = {}
-        grouped_of = {}
         quantised_of = {}
         sums_of = {}
-        for turn in range(N_SLOTS + 5):
+        for turn in range(N_SLOTS + 2):
             if turn < N_SLOTS:
                 planes_of[turn] = first_matmul(turn)
             if turn + 1 < N_GROUPS:
                 sort_w1_words(turn + 1)
             if turn < HALF_PAIRS:
                 quantise_h(HALF_PAIRS + turn)
-            if 0 <= turn - 4 < N_SLOTS:
-                half, g = divmod(turn - 4, N_GROUPS)
+            if 0 <= turn - 2 < N_SLOTS:
+                half, g = divmod(turn - 2, N_GROUPS)
                 if g == 0:
                     sums_of[half] = [
                         psum_s.tile([P, D_MODEL], F32, name="ff%d" % k, tag="shared")
                         for k in range(HALF_TILES)
                     ]
-                a_words, a_scales = quantised_of[turn - 4]
-                second_matmul(g, a_words, a_scales, sums_of[half])
-            if 0 <= turn - 2 < N_SLOTS:
-                grouped_of[turn - 2] = regroup_a(planes_of[turn - 2])
-            if 0 <= turn - 3 < N_SLOTS:
-                quantised_of[turn - 3] = quantise_a(grouped_of[turn - 3])
-            if closes_half(turn - 4):
-                add_residual((turn - 4) // N_GROUPS, sums_of[(turn - 4) // N_GROUPS])
-            if closes_half(turn - 5):
-                sum_squares((turn - 5) // N_GROUPS)
+                second_matmul(g, quantised_of[turn - 2], sums_of[half])
+            if 0 <= turn - 1 < N_SLOTS:
+                grouped = [regroup_a(planes_of[turn - 1], c) for c in range(HALF_CHUNKS)]
+                quantised_of[turn - 1] = [quantise_a(grouped[c]) for c in range(HALF_CHUNKS)]
+            if closes_half(turn - 2):
+                add_residual((turn - 2) // N_GROUPS, sums_of[(turn - 2) // N_GROUPS])
+            if turn == N_SLOTS - 1:
+                sum_squares(0)
+            if turn == N_SLOTS + 1:
+                sum_squares(1)
 
         totals = psum_s.tile([P, 2, N_TILES], F32, name="totals", tag="shared")
         nc.tensor.matmul(
@@ -329,13 +331,31 @@ def tile_decoderblock_pb_kernel(
         )
         nc.scalar.activation(out=std[:], in_=minus_var[:], func=ACT.Sqrt, scale=-1.0, bias=eps[:])
         nc.vector.reciprocal(out=rstd[:], in_=std[:])
+        nc.vector.tensor_scalar(
+            out=minus_mean_rstd[:],
+            in0=mean,
+            scalar1=rstd[:],
+            scalar2=-1.0,
+            op0=ALU.mult,
+            op1=ALU.mult,
+        )
         for i in range(N_TILES):
-            nc.vector.tensor_scalar(
-                out=t_sb[:, i, :],
-                in0=t_sb[:, i, :],
-                scalar1=mean,
-                scalar2=rstd[:],
-                op0=ALU.subtract,
-                op1=ALU.mult,
-            )
-            nc.sync.dma_start(out=out_rows[:, i, :], in_=t_sb[:, i, :])
+            if i in SCALAR_NORM_TILES:
+                nc.scalar.activation(
+                    out=t_sb[:, i, :],
+                    in_=t_sb[:, i, :],
+                    func=ACT.Identity,
+                    scale=rstd[:],
+                    bias=minus_mean_rstd[:],
+                )
+                nc.scalar.dma_start(out=out_rows[:, i, :], in_=t_sb[:, i, :])
+            else:
+                nc.vector.tensor_scalar(
+                    out=t_sb[:, i, :],
+                    in0=t_sb[:, i, :],
+                    scalar1=mean,
+                    scalar2=rstd[:],
+                    op0=ALU.subtract,
+                    op1=ALU.mult,
+                )
+                nc.sync.dma_start(out=out_rows[:, i, :], in_=t_sb[:, i, :])

@@ -34,7 +34,7 @@ HALF_CHUNKS = 2
 CHUNK_TILES = 2
 N_BLOCKS = D_FF // P
 N_SLOTS = N_HALVES * N_GROUPS
-FILL_TURNS = 1
+FILL_TURNS = 0
 SCALAR_NORM_TILES = (1, 4, 7)
 
 FLOPS = 2 * TOKENS * D_MODEL * D_FF * 2
@@ -272,10 +272,13 @@ def tile_decoderblock_pb_kernel(
         b2_bank = psum_s.tile([P, D_MODEL], F32, name="b2_bank", tag="shared")
         nc.tensor.matmul(out=b2_bank[:], lhsT=ones_bf[:], rhs=b2_rows[:], start=True, stop=True)
         nc.scalar.copy(out=b2_all[:], in_=b2_bank[:])
-        for i in range(N_TILES):
-            nc.gpsimd.tensor_tensor(
+        def add_b2(i):
+            nc.vector.tensor_tensor(
                 out=h_plus_b2[:, i, :], in0=h_sb[:, i, :], in1=b2_all[:], op=ALU.add
             )
+
+        for i in range(HALF_TILES):
+            add_b2(i)
 
         def closes_half(slot):
             return 0 <= slot < N_SLOTS and slot % N_GROUPS == N_GROUPS - 1
@@ -301,6 +304,8 @@ def tile_decoderblock_pb_kernel(
             if 0 <= turn - 1 < N_SLOTS:
                 grouped = [regroup_a(planes_of[turn - 1], c) for c in range(HALF_CHUNKS)]
                 quantised_of[turn - 1] = [quantise_a(grouped[c]) for c in range(HALF_CHUNKS)]
+            if 1 <= turn <= HALF_TILES:
+                add_b2(HALF_TILES + turn - 1)
             if closes_half(turn - 2):
                 add_residual((turn - 2) // N_GROUPS, sums_of[(turn - 2) // N_GROUPS])
             if turn == N_SLOTS - 1:

@@ -34,7 +34,75 @@ HALF_CHUNKS = 2
 CHUNK_TILES = 2
 N_BLOCKS = D_FF // P
 N_SLOTS = N_HALVES * N_GROUPS
-FILL_TURNS = 0
+UNITS = ((0, 512, 0), (0, 512, 1), (0, 512, 2), (0, 512, 3), (512, 512, 0), (512, 512, 1), (512, 512, 2), (512, 256, 3), (768, 256, 3))
+VECTOR_TAKES = ((1, 3), (2, 3), (3, 3))
+PLAN = [
+    ("hb", 0),
+    ("hb", 1),
+    ("first", 0),
+    ("sort", 1),
+    ("sort", 2),
+    ("sort", 3),
+    ("h", 2),
+    ("h", 3),
+    ("hb", 2),
+    ("first", 1),
+    ("regroup", 0),
+    ("quantise", 0),
+    ("hb", 3),
+    ("first", 2),
+    ("second", 0),
+    ("regroup", 1),
+    ("quantise", 1),
+    ("hb", 4),
+    ("first", 3),
+    ("second", 1),
+    ("regroup", 2),
+    ("quantise", 2),
+    ("hb", 5),
+    ("first", 4),
+    ("second", 2),
+    ("regroup", 3),
+    ("quantise", 3),
+    ("hb", 6),
+    ("first", 5),
+    ("second", 3),
+    ("regroup", 4),
+    ("quantise", 4),
+    ("hb", 7),
+    ("t", 0),
+    ("t", 1),
+    ("t", 2),
+    ("t", 3),
+    ("first", 6),
+    ("second", 4),
+    ("regroup", 5),
+    ("quantise", 5),
+    ("first", 7),
+    ("first", 8),
+    ("second", 5),
+    ("regroup", 6),
+    ("quantise", 6),
+    ("sq", 0),
+    ("sq", 1),
+    ("sq", 2),
+    ("sq", 3),
+    ("second", 6),
+    ("regroup", 7),
+    ("quantise", 7),
+    ("second", 7),
+    ("regroup", 8),
+    ("quantise", 8),
+    ("second", 8),
+    ("t", 4),
+    ("t", 5),
+    ("t", 6),
+    ("t", 7),
+    ("sq", 4),
+    ("sq", 5),
+    ("sq", 6),
+    ("sq", 7),
+]
 SCALAR_NORM_TILES = (1, 4, 7)
 
 FLOPS = 2 * TOKENS * D_MODEL * D_FF * 2
@@ -55,7 +123,6 @@ def tile_decoderblock_pb_kernel(
         keep = ctx.enter_context(tc.tile_pool(name="keep", bufs=1))
         ring3 = ctx.enter_context(tc.tile_pool(name="ring3", bufs=3))
         ring4 = ctx.enter_context(tc.tile_pool(name="ring4", bufs=4))
-        ring6 = ctx.enter_context(tc.tile_pool(name="ring6", bufs=6))
         psum_x = ctx.enter_context(tc.psum_pool(name="psum_x", bufs=4))
         psum_s = ctx.enter_context(tc.psum_pool(name="psum_s", bufs=4))
         ctx.enter_context(tc.manual_schedule())
@@ -80,7 +147,6 @@ def tile_decoderblock_pb_kernel(
         b1_sorted = keep.tile([P, K_PASS], BF16)
         b1_cols = keep.tile([P, N_BLOCKS], F32)
         b2_rows = keep.tile([P, D_MODEL], BF16)
-        b2_all = keep.tile([P, D_MODEL], BF16)
         h_plus_b2 = keep.tile([P, N_TILES, D_MODEL], F32)
         t_sb = keep.tile([P, N_TILES, D_MODEL], F32)
         squares = keep.tile([P, D_MODEL], BF16)
@@ -143,6 +209,11 @@ def tile_decoderblock_pb_kernel(
                 in_=w_ff2_words[g].rearrange("p n t -> p (n t)").bitcast(I32),
             )
 
+        planes_of = {}
+        grouped_of = {}
+        quantised_of = {}
+        sums_of = {}
+
         def quantise_h(pair):
             bank = psum_s.tile([P, 2, PAIR * P], F32, name="h_bank", tag="shared")
             for j in range(PAIR):
@@ -170,22 +241,23 @@ def tile_decoderblock_pb_kernel(
                 in_=w1_words_given[:, block(g, K_PASS)].bitcast(I32).rearrange(AS_GIVEN, t=PACK),
             )
 
-        def first_matmul(slot):
-            half, g = divmod(slot, N_GROUPS)
-            a_planes = ring3.tile([P, PACK, HALF], BF16, name="a_planes")
+        def first_matmul(unit):
+            first, tokens, g = UNITS[unit]
+            columns = slice(first, first + tokens)
+            a_planes = ring3.tile([P, PACK, tokens], BF16, name="a_planes")
             for t in range(PACK):
                 j = PACK * g + t
-                x = psum_x.tile([P, HALF], F32, name="x")
+                x = psum_x.tile([P, tokens], F32, name="x")
                 nc.tensor.matmul_mx(
                     out=x[:],
                     lhsT=w1_words[:, block(j, P)].bitcast(FP8X4),
                     lhsT_scale=w1_scales[4 * g : P, block(t, P)],
-                    rhs=h_words[:, block(half, HALF)].bitcast(FP8X4),
-                    rhs_scale=h_scales[:, block(half, HALF)],
+                    rhs=h_words[:, columns].bitcast(FP8X4),
+                    rhs_scale=h_scales[:, columns],
                     start=True,
                     stop=True,
                 )
-                if slot < FILL_TURNS and t % 2 == 1:
+                if (unit, t) in VECTOR_TAKES:
                     nc.vector.tensor_scalar(
                         out=a_planes[:, t, :],
                         in0=x[:],
@@ -198,58 +270,61 @@ def tile_decoderblock_pb_kernel(
                     nc.scalar.activation(
                         out=a_planes[:, t, :], in_=x[:], func=ACT.Relu, bias=b1_cols[:, j : j + 1]
                     )
-            return a_planes
+            planes_of[unit] = a_planes
 
-        def regroup_a(a_planes, c):
-            grouped = ring4.tile([P, PACK * CHUNK], BF16, name="grouped", align_bytes=64)
+        def regroup_a(unit):
+            tokens = UNITS[unit][1]
+            grouped = ring3.tile([P, PACK * tokens], BF16, name="grouped", align_bytes=64)
             nc.vector.tensor_copy(
                 out=grouped[:].rearrange("p (c i t) -> p c t i", i=4, t=PACK),
-                in_=a_planes[:, :, block(c, CHUNK)].rearrange("p t (c i) -> p c t i", i=4),
+                in_=planes_of[unit][:].rearrange("p t (c i) -> p c t i", i=4),
             )
-            return grouped
+            grouped_of[unit] = grouped
 
-        def quantise_a(grouped):
-            a_words = ring6.tile([P, CHUNK], U32, name="a_words", align_bytes=64)
-            a_scales = ring6.tile([P, CHUNK], U8, name="a_scales", align_bytes=64)
+        def quantise_a(unit):
+            tokens = UNITS[unit][1]
+            a_words = ring4.tile([P, tokens], U32, name="a_words", align_bytes=64)
+            a_scales = ring4.tile([P, tokens], U8, name="a_scales", align_bytes=64)
             nc.vector.quantize_mx(
-                out=a_words[:].bitcast(FP8X4), scales=a_scales[:], in_=grouped[:]
+                out=a_words[:].bitcast(FP8X4), scales=a_scales[:], in_=grouped_of[unit][:]
             )
-            return a_words, a_scales
+            quantised_of[unit] = (a_words, a_scales)
 
-        def second_matmul(g, quantised, sums):
-            for k in range(HALF_TILES):
-                a_words, a_scales = quantised[k // CHUNK_TILES]
+        def second_matmul(unit):
+            first, tokens, g = UNITS[unit]
+            a_words, a_scales = quantised_of[unit]
+            for k in range(tokens // P):
+                i = first // P + k
+                if g == 0:
+                    sums_of[i] = psum_s.tile([P, D_MODEL], F32, name="ff", tag="shared")
                 nc.tensor.matmul_mx(
-                    out=sums[k][:],
-                    lhsT=a_words[:, block(k % CHUNK_TILES, P)].bitcast(FP8X4),
-                    lhsT_scale=a_scales[:, block(k % CHUNK_TILES, P)],
+                    out=sums_of[i][:],
+                    lhsT=a_words[:, block(k, P)].bitcast(FP8X4),
+                    lhsT_scale=a_scales[:, block(k, P)],
                     rhs=w2_words[:, g, :].bitcast(FP8X4),
                     rhs_scale=w2_scales[4 * g : P, :],
                     start=(g == 0),
                     stop=(g == N_GROUPS - 1),
                 )
 
-        def add_residual(half, sums):
-            for k in range(HALF_TILES):
-                i = HALF_TILES * half + k
-                nc.vector.scalar_tensor_tensor(
-                    out=t_sb[:, i, :],
-                    in0=sums[k][:],
-                    scalar=1.0,
-                    in1=h_plus_b2[:, i, :],
-                    op0=ALU.mult,
-                    op1=ALU.add,
-                    accum_out=t_sums[:, 0, i : i + 1],
-                )
+        def add_residual(i):
+            nc.vector.scalar_tensor_tensor(
+                out=t_sb[:, i, :],
+                in0=sums_of[i][:],
+                scalar=1.0,
+                in1=h_plus_b2[:, i, :],
+                op0=ALU.mult,
+                op1=ALU.add,
+                accum_out=t_sums[:, 0, i : i + 1],
+            )
 
-        def sum_squares(half):
-            for i in range(HALF_TILES * half, HALF_TILES * (half + 1)):
-                nc.scalar.activation(
-                    out=squares[:],
-                    in_=t_sb[:, i, :],
-                    func=ACT.Square,
-                    accum_out=t_sums[:, 1, i : i + 1],
-                )
+        def sum_squares(i):
+            nc.scalar.activation(
+                out=squares[:],
+                in_=t_sb[:, i, :],
+                func=ACT.Square,
+                accum_out=t_sums[:, 1, i : i + 1],
+            )
 
         nc.vector.tensor_copy(
             out=b1_sorted[:].rearrange(SORTED, t=PACK),
@@ -269,49 +344,34 @@ def tile_decoderblock_pb_kernel(
         nc.vector.tensor_copy(
             out=b1_cols[:].rearrange("p (g t) -> p t g", t=PACK), in_=b1_bank[:, :, 0:N_GROUPS]
         )
-        b2_bank = psum_s.tile([P, D_MODEL], F32, name="b2_bank", tag="shared")
-        nc.tensor.matmul(out=b2_bank[:], lhsT=ones_bf[:], rhs=b2_rows[:], start=True, stop=True)
-        nc.scalar.copy(out=b2_all[:], in_=b2_bank[:])
         def add_b2(i):
-            nc.vector.tensor_tensor(
-                out=h_plus_b2[:, i, :], in0=h_sb[:, i, :], in1=b2_all[:], op=ALU.add
+            bank = psum_x.tile([P, D_MODEL], F32, name="x")
+            nc.tensor.matmul(
+                out=bank[:], lhsT=identity_bf[:], rhs=h_sb[:, i, :], start=True, stop=False
             )
+            nc.tensor.matmul(out=bank[:], lhsT=ones_bf[:], rhs=b2_rows[:], start=False, stop=True)
+            nc.scalar.copy(out=h_plus_b2[:, i, :], in_=bank[:])
 
-        for i in range(HALF_TILES):
-            add_b2(i)
-
-        def closes_half(slot):
-            return 0 <= slot < N_SLOTS and slot % N_GROUPS == N_GROUPS - 1
-
-        planes_of = {}
-        quantised_of = {}
-        sums_of = {}
-        for turn in range(N_SLOTS + 2):
-            if turn < N_SLOTS:
-                planes_of[turn] = first_matmul(turn)
-            if turn + 1 < N_GROUPS:
-                sort_w1_words(turn + 1)
-            if turn < HALF_PAIRS:
-                quantise_h(HALF_PAIRS + turn)
-            if 0 <= turn - 2 < N_SLOTS:
-                half, g = divmod(turn - 2, N_GROUPS)
-                if g == 0:
-                    sums_of[half] = [
-                        psum_s.tile([P, D_MODEL], F32, name="ff%d" % k, tag="shared")
-                        for k in range(HALF_TILES)
-                    ]
-                second_matmul(g, quantised_of[turn - 2], sums_of[half])
-            if 0 <= turn - 1 < N_SLOTS:
-                grouped = [regroup_a(planes_of[turn - 1], c) for c in range(HALF_CHUNKS)]
-                quantised_of[turn - 1] = [quantise_a(grouped[c]) for c in range(HALF_CHUNKS)]
-            if 1 <= turn <= HALF_TILES:
-                add_b2(HALF_TILES + turn - 1)
-            if closes_half(turn - 2):
-                add_residual((turn - 2) // N_GROUPS, sums_of[(turn - 2) // N_GROUPS])
-            if turn == N_SLOTS - 1:
-                sum_squares(0)
-            if turn == N_SLOTS + 1:
-                sum_squares(1)
+        for step in PLAN:
+            job, arg = step
+            if job == "first":
+                first_matmul(arg)
+            elif job == "sort":
+                sort_w1_words(arg)
+            elif job == "h":
+                quantise_h(arg)
+            elif job == "hb":
+                add_b2(arg)
+            elif job == "regroup":
+                regroup_a(arg)
+            elif job == "quantise":
+                quantise_a(arg)
+            elif job == "second":
+                second_matmul(arg)
+            elif job == "t":
+                add_residual(arg)
+            elif job == "sq":
+                sum_squares(arg)
 
         totals = psum_s.tile([P, 2, N_TILES], F32, name="totals", tag="shared")
         nc.tensor.matmul(

@@ -35,63 +35,64 @@ CHUNK_TILES = 2
 N_BLOCKS = D_FF // P
 N_SLOTS = N_HALVES * N_GROUPS
 UNITS = ((0, 512, 0), (0, 512, 1), (0, 512, 2), (0, 512, 3), (512, 512, 0), (512, 512, 1), (512, 512, 2), (512, 256, 3), (768, 256, 3))
-VECTOR_TAKES = ((1, 3), (2, 3), (3, 3))
+VECTOR_TAKES = ()
 PLAN = [
-    ("hb", 0),
-    ("hb", 1),
+    ("b2", 0),
     ("first", 0),
     ("sort", 1),
     ("sort", 2),
     ("sort", 3),
-    ("h", 2),
-    ("h", 3),
-    ("hb", 2),
+    ("ht", 2),
+    ("ht", 3),
+    ("hq", 2),
+    ("hq", 3),
     ("first", 1),
     ("regroup", 0),
+    ("hbv", 0),
     ("quantise", 0),
-    ("hb", 3),
     ("first", 2),
     ("second", 0),
     ("regroup", 1),
+    ("hbv", 1),
     ("quantise", 1),
-    ("hb", 4),
     ("first", 3),
     ("second", 1),
     ("regroup", 2),
+    ("hbv", 2),
     ("quantise", 2),
-    ("hb", 5),
     ("first", 4),
     ("second", 2),
     ("regroup", 3),
+    ("hbv", 3),
     ("quantise", 3),
-    ("hb", 6),
     ("first", 5),
     ("second", 3),
     ("regroup", 4),
-    ("quantise", 4),
-    ("hb", 7),
     ("t", 0),
     ("t", 1),
+    ("quantise", 4),
     ("t", 2),
     ("t", 3),
     ("first", 6),
     ("second", 4),
     ("regroup", 5),
+    ("hbv", 4),
     ("quantise", 5),
+    ("sq2", 0),
     ("first", 7),
     ("first", 8),
     ("second", 5),
     ("regroup", 6),
+    ("hbv", 5),
     ("quantise", 6),
-    ("sq", 0),
-    ("sq", 1),
-    ("sq", 2),
-    ("sq", 3),
+    ("sq2", 2),
     ("second", 6),
     ("regroup", 7),
+    ("hbv", 6),
     ("quantise", 7),
     ("second", 7),
     ("regroup", 8),
+    ("hbv", 7),
     ("quantise", 8),
     ("second", 8),
     ("t", 4),
@@ -149,24 +150,24 @@ def tile_decoderblock_pb_kernel(
         b2_rows = keep.tile([P, D_MODEL], BF16)
         h_plus_b2 = keep.tile([P, N_TILES, D_MODEL], F32)
         t_sb = keep.tile([P, N_TILES, D_MODEL], F32)
-        squares = keep.tile([P, D_MODEL], BF16)
+        squares = keep.tile([P, 2 * D_MODEL], BF16)
+        b2_all = keep.tile([P, D_MODEL], BF16)
         t_sums = keep.tile([P, 2, N_TILES], F32)
-        moments = keep.tile([P, 2], F32)
+        mean = keep.tile([P, 1], F32)
         minus_var = keep.tile([P, 1], F32)
-        std = keep.tile([P, 1], F32)
         rstd = keep.tile([P, 1], F32)
-        minus_mean_rstd = keep.tile([P, 1], F32)
 
         nc.vector.memset(b1_given[:].bitcast(I32), 0)
         nc.vector.memset(w1_scales_given[:].bitcast(I32), 0)
         nc.vector.memset(b2_rows[:].bitcast(I32), 0)
         nc.vector.memset(w2_scales[:].bitcast(I32), 0)
+        nc.vector.memset(t_sums[:], 0.0)
         nc.vector.memset(ones_bf[:], 1.0)
         nc.vector.memset(eps[:], EPS)
         nc.vector.memset(mean_weights[:], 1.0 / (TOKENS * D_MODEL))
         make_identity(nc, identity[:])
         make_identity(nc, identity_bf[:])
-        nc.scalar.activation(out=table_warmer[:], in_=eps[:], func=ACT.Sqrt)
+        nc.scalar.activation(out=table_warmer[:], in_=eps[:], func=ACT.Abs_reciprocal_sqrt)
 
         def load_h(pair):
             tiles = block(pair, PAIR)
@@ -214,7 +215,7 @@ def tile_decoderblock_pb_kernel(
         quantised_of = {}
         sums_of = {}
 
-        def quantise_h(pair):
+        def turn_h(pair):
             bank = psum_s.tile([P, 2, PAIR * P], F32, name="h_bank", tag="shared")
             for j in range(PAIR):
                 words = h_sb[:, PAIR * pair + j, :].bitcast(F32)
@@ -229,6 +230,8 @@ def tile_decoderblock_pb_kernel(
                 .rearrange("p (c u) -> p c u", u=2),
                 in_=bank[:].rearrange("p u c -> p c u"),
             )
+
+        def quantise_h(pair):
             nc.vector.quantize_mx(
                 out=h_words[:, block(pair, PAIR * P)].bitcast(FP8X4),
                 scales=h_scales[:, block(pair, PAIR * P)],
@@ -320,7 +323,7 @@ def tile_decoderblock_pb_kernel(
 
         def sum_squares(i):
             nc.scalar.activation(
-                out=squares[:],
+                out=squares[:, 0:D_MODEL],
                 in_=t_sb[:, i, :],
                 func=ACT.Square,
                 accum_out=t_sums[:, 1, i : i + 1],
@@ -331,13 +334,14 @@ def tile_decoderblock_pb_kernel(
             in_=b1_given[:].rearrange(AS_GIVEN, t=PACK),
         )
         nc.vector.tensor_copy(
-            out=w1_scales[:].rearrange("p (t m) -> p m t", t=PACK),
-            in_=w1_scales_given[:].rearrange("p (m t) -> p m t", t=PACK),
+            out=w1_scales[:].rearrange(SORTED, t=PACK),
+            in_=w1_scales_given[:].rearrange(AS_GIVEN, t=PACK),
         )
+        turn_h(0)
         quantise_h(0)
         sort_w1_words(0)
-        for pair in range(1, HALF_PAIRS):
-            quantise_h(pair)
+        turn_h(1)
+        quantise_h(1)
         b1_bank = psum_s.tile([P, PACK, P], BF16, name="b1_bank", tag="shared")
         for t in range(PACK):
             nc.tensor.transpose(b1_bank[:, t, :], b1_sorted[:, block(t, P)], identity_bf[:])
@@ -352,13 +356,33 @@ def tile_decoderblock_pb_kernel(
             nc.tensor.matmul(out=bank[:], lhsT=ones_bf[:], rhs=b2_rows[:], start=False, stop=True)
             nc.scalar.copy(out=h_plus_b2[:, i, :], in_=bank[:])
 
+        def spread_b2():
+            bank = psum_x.tile([P, D_MODEL], F32, name="x")
+            nc.tensor.matmul(out=bank[:], lhsT=ones_bf[:], rhs=b2_rows[:], start=True, stop=True)
+            nc.scalar.copy(out=b2_all[:], in_=bank[:])
+
+        def add_b2_on_vector(i):
+            nc.vector.tensor_tensor(
+                out=h_plus_b2[:, i, :], in0=h_sb[:, i, :], in1=b2_all[:], op=ALU.add
+            )
+
+        def sum_squares_of_two(i):
+            nc.scalar.activation(
+                out=squares[:],
+                in_=t_sb[:, i : i + 2, :].rearrange("p i d -> p (i d)"),
+                func=ACT.Square,
+                accum_out=t_sums[:, 1, i : i + 1],
+            )
+
         for step in PLAN:
             job, arg = step
             if job == "first":
                 first_matmul(arg)
             elif job == "sort":
                 sort_w1_words(arg)
-            elif job == "h":
+            elif job == "ht":
+                turn_h(arg)
+            elif job == "hq":
                 quantise_h(arg)
             elif job == "hb":
                 add_b2(arg)
@@ -372,55 +396,41 @@ def tile_decoderblock_pb_kernel(
                 add_residual(arg)
             elif job == "sq":
                 sum_squares(arg)
+            elif job == "sq2":
+                sum_squares_of_two(arg)
+            elif job == "b2":
+                spread_b2()
+            elif job == "hbv":
+                add_b2_on_vector(arg)
 
-        totals = psum_s.tile([P, 2, N_TILES], F32, name="totals", tag="shared")
-        nc.tensor.matmul(
-            out=totals[:].rearrange("p s i -> p (s i)"),
-            lhsT=mean_weights[:],
-            rhs=t_sums[:].rearrange("p s i -> p (s i)"),
-            start=True,
-            stop=True,
-        )
-        nc.vector.tensor_reduce(
-            out=moments[:], in_=totals[:], axis=mybir.AxisListType.X, op=ALU.add
-        )
-        mean = moments[:, 0:1]
-        mean_of_squares = moments[:, 1:2]
-        nc.vector.scalar_tensor_tensor(
+        totals = psum_s.tile([P, 2], F32, name="totals", tag="shared")
+        for i in range(N_TILES):
+            nc.tensor.matmul(
+                out=totals[:],
+                lhsT=mean_weights[:],
+                rhs=t_sums[:, :, i],
+                start=(i == 0),
+                stop=(i == N_TILES - 1),
+            )
+        nc.vector.tensor_scalar(
             out=minus_var[:],
-            in0=mean,
-            scalar=mean,
-            in1=mean_of_squares,
+            in0=totals[:, 0:1],
+            scalar1=totals[:, 0:1],
+            scalar2=totals[:, 1:2],
             op0=ALU.mult,
             op1=ALU.subtract,
         )
-        nc.scalar.activation(out=std[:], in_=minus_var[:], func=ACT.Sqrt, scale=-1.0, bias=eps[:])
-        nc.vector.reciprocal(out=rstd[:], in_=std[:])
-        nc.vector.tensor_scalar(
-            out=minus_mean_rstd[:],
-            in0=mean,
-            scalar1=rstd[:],
-            scalar2=-1.0,
-            op0=ALU.mult,
-            op1=ALU.mult,
+        nc.scalar.activation(
+            out=rstd[:], in_=minus_var[:], func=ACT.Abs_reciprocal_sqrt, scale=-1.0, bias=eps[:]
         )
+        nc.vector.tensor_copy(out=mean[:], in_=totals[:, 0:1])
         for i in range(N_TILES):
-            if i in SCALAR_NORM_TILES:
-                nc.scalar.activation(
-                    out=t_sb[:, i, :],
-                    in_=t_sb[:, i, :],
-                    func=ACT.Identity,
-                    scale=rstd[:],
-                    bias=minus_mean_rstd[:],
-                )
-                nc.scalar.dma_start(out=out_rows[:, i, :], in_=t_sb[:, i, :])
-            else:
-                nc.vector.tensor_scalar(
-                    out=t_sb[:, i, :],
-                    in0=t_sb[:, i, :],
-                    scalar1=mean,
-                    scalar2=rstd[:],
-                    op0=ALU.subtract,
-                    op1=ALU.mult,
-                )
-                nc.sync.dma_start(out=out_rows[:, i, :], in_=t_sb[:, i, :])
+            nc.vector.tensor_scalar(
+                out=t_sb[:, i, :],
+                in0=t_sb[:, i, :],
+                scalar1=mean[:],
+                scalar2=rstd[:],
+                op0=ALU.subtract,
+                op1=ALU.mult,
+            )
+            nc.sync.dma_start(out=out_rows[:, i, :], in_=t_sb[:, i, :])

@@ -85,14 +85,14 @@ PLAN = [
     ("regroup", 6),
     ("hbv", 5),
     ("quantise", 6),
+    ("hb", 6),
+    ("hb", 7),
     ("sq2", 2),
     ("second", 6),
     ("regroup", 7),
-    ("hbv", 6),
+    ("regroup", 8),
     ("quantise", 7),
     ("second", 7),
-    ("regroup", 8),
-    ("hbv", 7),
     ("quantise", 8),
     ("second", 8),
     ("t", 4),
@@ -412,6 +412,7 @@ def tile_decoderblock_pb_kernel(
                 start=(i == 0),
                 stop=(i == N_TILES - 1),
             )
+        nc.vector.tensor_copy(out=mean[:], in_=totals[:, 0:1])
         nc.vector.tensor_scalar(
             out=minus_var[:],
             in0=totals[:, 0:1],
@@ -423,7 +424,6 @@ def tile_decoderblock_pb_kernel(
         nc.scalar.activation(
             out=rstd[:], in_=minus_var[:], func=ACT.Abs_reciprocal_sqrt, scale=-1.0, bias=eps[:]
         )
-        nc.vector.tensor_copy(out=mean[:], in_=totals[:, 0:1])
         for i in range(N_TILES):
             nc.vector.tensor_scalar(
                 out=t_sb[:, i, :],

@@ -36,24 +36,25 @@ N_BLOCKS = D_FF // P
 N_SLOTS = N_HALVES * N_GROUPS
 UNITS = ((0, 512, 0), (0, 512, 1), (0, 512, 2), (0, 512, 3), (512, 512, 0), (512, 512, 1), (512, 512, 2), (512, 256, 3), (768, 256, 3))
 VECTOR_TAKES = ()
+SCALAR_TURNS = (0, 1)
 PLAN = [
     ("b2", 0),
     ("first", 0),
     ("sort", 1),
     ("sort", 2),
     ("sort", 3),
+    ("hbv", 0),
+    ("hbv", 1),
     ("ht", 2),
     ("ht", 3),
-    ("hq", 2),
-    ("hq", 3),
     ("first", 1),
     ("regroup", 0),
-    ("hbv", 0),
+    ("hq", 2),
     ("quantise", 0),
     ("first", 2),
     ("second", 0),
     ("regroup", 1),
-    ("hbv", 1),
+    ("hq", 3),
     ("quantise", 1),
     ("first", 3),
     ("second", 1),
@@ -223,7 +224,7 @@ def tile_decoderblock_pb_kernel(
                     nc.tensor.transpose(
                         bank[:, u, block(j, P)], words[:, u : D_MODEL // 2 : 2], identity[:]
                     )
-            copy = nc.scalar.copy if pair < HALF_PAIRS else nc.vector.tensor_copy
+            copy = nc.scalar.copy if pair in SCALAR_TURNS else nc.vector.tensor_copy
             copy(
                 out=h_grouped[:, block(pair, PAIR * K_PASS)]
                 .bitcast(F32)

@@ -37,6 +37,7 @@ N_SLOTS = N_HALVES * N_GROUPS
 UNITS = ((0, 512, 0), (0, 512, 1), (0, 512, 2), (0, 512, 3), (512, 512, 0), (512, 512, 1), (512, 512, 2), (512, 256, 3), (768, 256, 3))
 VECTOR_TAKES = ()
 SCALAR_TURNS = (0, 1)
+STORE_TILES = (1, 1, 2, 2, 2)
 PLAN = [
     ("b2", 0),
     ("first", 0),
@@ -425,13 +426,17 @@ def tile_decoderblock_pb_kernel(
         nc.scalar.activation(
             out=rstd[:], in_=minus_var[:], func=ACT.Abs_reciprocal_sqrt, scale=-1.0, bias=eps[:]
         )
-        for i in range(N_TILES):
-            nc.vector.tensor_scalar(
-                out=t_sb[:, i, :],
-                in0=t_sb[:, i, :],
-                scalar1=mean[:],
-                scalar2=rstd[:],
-                op0=ALU.subtract,
-                op1=ALU.mult,
-            )
-            nc.sync.dma_start(out=out_rows[:, i, :], in_=t_sb[:, i, :])
+        first_of_store = 0
+        for tiles in STORE_TILES:
+            for i in range(first_of_store, first_of_store + tiles):
+                nc.vector.tensor_scalar(
+                    out=t_sb[:, i, :],
+                    in0=t_sb[:, i, :],
+                    scalar1=mean[:],
+                    scalar2=rstd[:],
+                    op0=ALU.subtract,
+                    op1=ALU.mult,
+                )
+            stored = slice(first_of_store, first_of_store + tiles)
+            nc.sync.dma_start(out=out_rows[:, stored, :], in_=t_sb[:, stored, :])
+            first_of_store += tiles

@@ -242,8 +242,8 @@ def tile_decoderblock_pb_kernel(
 
         def sort_w1_words(g):
             nc.vector.tensor_copy(
-                out=w1_words[:, block(g, K_PASS)].bitcast(I32).rearrange(SORTED, t=PACK),
-                in_=w1_words_given[:, block(g, K_PASS)].bitcast(I32).rearrange(AS_GIVEN, t=PACK),
+                out=w1_words[:, block(g, K_PASS)].bitcast(I32).rearrange("p (t m) -> p m t", t=PACK),
+                in_=w1_words_given[:, block(g, K_PASS)].bitcast(I32).rearrange("p (m t) -> p m t", t=PACK),
             )
 
         def first_matmul(unit):

@@ -427,7 +427,7 @@ def tile_decoderblock_pb_kernel(
             out=rstd[:], in_=minus_var[:], func=ACT.Abs_reciprocal_sqrt, scale=-1.0, bias=eps[:]
         )
         first_of_store = 0
-        for tiles in STORE_TILES:
+        for n, tiles in enumerate(STORE_TILES):
             for i in range(first_of_store, first_of_store + tiles):
                 nc.vector.tensor_scalar(
                     out=t_sb[:, i, :],
@@ -438,5 +438,6 @@ def tile_decoderblock_pb_kernel(
                     op1=ALU.mult,
                 )
             stored = slice(first_of_store, first_of_store + tiles)
-            nc.sync.dma_start(out=out_rows[:, stored, :], in_=t_sb[:, stored, :])
+            queue = nc.sync if n % 2 == 0 else nc.scalar
+            queue.dma_start(out=out_rows[:, stored, :], in_=t_sb[:, stored, :])
             first_of_store += tiles

from contextlib import ExitStack

import concourse.mybir as mybir
from concourse.masks import make_identity

F32 = mybir.dt.float32
BF16 = mybir.dt.bfloat16
I32 = mybir.dt.int32
U32 = mybir.dt.uint32
U8 = mybir.dt.uint8
FP8X4 = mybir.dt.float8_e4m3fn_x4
ALU = mybir.AluOpType
ACT = mybir.ActivationFunctionType

P = 128
PACK = 4
K_PASS = PACK * P
TOKENS = 1024
D_MODEL = 512
D_FF = 2048
EPS = 1e-5
N_TILES = TOKENS // P
N_HALVES = 2
HALF = TOKENS // N_HALVES
HALF_TILES = HALF // P
PAIR = 2
HALF_PAIRS = HALF_TILES // PAIR
N_GROUPS = D_FF // K_PASS
QUADS = K_PASS // P
AS_GIVEN = "p (m t) -> p t m"
SORTED = "p (t m) -> p t m"
CHUNK = 256
HALF_CHUNKS = 2
CHUNK_TILES = 2
N_BLOCKS = D_FF // P
N_SLOTS = N_HALVES * N_GROUPS
UNITS = ((0, 512, 0), (0, 512, 1), (0, 512, 2), (0, 512, 3), (512, 512, 0), (512, 512, 1), (512, 512, 2), (512, 256, 3), (768, 256, 3))
VECTOR_TAKES = ()
SCALAR_TURNS = (0, 1)
STORE_TILES = (1, 1, 2, 2, 2)
PLAN = [
    ("b2", 0),
    ("first", 0),
    ("sort", 1),
    ("sort", 2),
    ("sort", 3),
    ("hbv", 0),
    ("hbv", 1),
    ("ht", 2),
    ("ht", 3),
    ("first", 1),
    ("regroup", 0),
    ("hq", 2),
    ("quantise", 0),
    ("first", 2),
    ("second", 0),
    ("regroup", 1),
    ("hq", 3),
    ("quantise", 1),
    ("first", 3),
    ("second", 1),
    ("regroup", 2),
    ("hbv", 2),
    ("quantise", 2),
    ("first", 4),
    ("second", 2),
    ("regroup", 3),
    ("hbv", 3),
    ("quantise", 3),
    ("first", 5),
    ("second", 3),
    ("regroup", 4),
    ("t", 0),
    ("t", 1),
    ("quantise", 4),
    ("t", 2),
    ("t", 3),
    ("first", 6),
    ("second", 4),
    ("regroup", 5),
    ("hbv", 4),
    ("quantise", 5),
    ("sq2", 0),
    ("first", 7),
    ("first", 8),
    ("second", 5),
    ("regroup", 6),
    ("hbv", 5),
    ("quantise", 6),
    ("hb", 6),
    ("hb", 7),
    ("sq2", 2),
    ("second", 6),
    ("regroup", 7),
    ("regroup", 8),
    ("quantise", 7),
    ("second", 7),
    ("quantise", 8),
    ("second", 8),
    ("t", 4),
    ("t", 5),
    ("t", 6),
    ("t", 7),
    ("sq", 4),
    ("sq", 5),
    ("sq", 6),
    ("sq", 7),
]
SCALAR_NORM_TILES = (1, 4, 7)

FLOPS = 2 * TOKENS * D_MODEL * D_FF * 2


def block(index, width):
    return slice(index * width, (index + 1) * width)


def tile_decoderblock_pb_kernel(
    tc, h2, w_ff1_words, w_ff1_scales, b_ff1, w_ff2_words, w_ff2_scales, b_ff2, out
):
    nc = tc.nc
    h_rows = h2.flatten_outer_dims().rearrange("(p i) d -> p i d", i=N_TILES)
    out_rows = out.flatten_outer_dims().rearrange("(p i) d -> p i d", i=N_TILES)

    with ExitStack() as ctx:
        keep = ctx.enter_context(tc.tile_pool(name="keep", bufs=1))
        ring3 = ctx.enter_context(tc.tile_pool(name="ring3", bufs=3))
        ring4 = ctx.enter_context(tc.tile_pool(name="ring4", bufs=4))
        psum_x = ctx.enter_context(tc.psum_pool(name="psum_x", bufs=4))
        psum_s = ctx.enter_context(tc.psum_pool(name="psum_s", bufs=4))
        ctx.enter_context(tc.manual_schedule())

        identity = keep.tile([P, P], F32)
        identity_bf = keep.tile([P, P], BF16)
        ones_bf = keep.tile([P, P], BF16)
        mean_weights = keep.tile([P, P], F32)
        eps = keep.tile([P, 1], F32)
        table_warmer = keep.tile([P, 1], F32)
        h_sb = keep.tile([P, N_TILES, D_MODEL], BF16)
        h_grouped = keep.tile([P, N_TILES * K_PASS], BF16, align_bytes=64)
        h_words = keep.tile([P, TOKENS], U32, align_bytes=64)
        h_scales = keep.tile([P, TOKENS], U8, align_bytes=64)
        w1_words_given = keep.tile([P, D_FF], U32)
        w1_scales_given = keep.tile([P, K_PASS], U8)
        w1_words = keep.tile([P, D_FF], U32, align_bytes=64)
        w1_scales = keep.tile([P, K_PASS], U8, align_bytes=64)
        w2_words = keep.tile([P, N_GROUPS, D_MODEL], U32, align_bytes=64)
        w2_scales = keep.tile([P, D_MODEL], U8, align_bytes=64)
        b1_given = keep.tile([P, K_PASS], BF16)
        b1_sorted = keep.tile([P, K_PASS], BF16)
        b1_cols = keep.tile([P, N_BLOCKS], F32)
        b2_rows = keep.tile([P, D_MODEL], BF16)
        h_plus_b2 = keep.tile([P, N_TILES, D_MODEL], F32)
        t_sb = keep.tile([P, N_TILES, D_MODEL], F32)
        squares = keep.tile([P, 2 * D_MODEL], BF16)
        b2_all = keep.tile([P, D_MODEL], BF16)
        t_sums = keep.tile([P, 2, N_TILES], F32)
        mean = keep.tile([P, 1], F32)
        minus_var = keep.tile([P, 1], F32)
        rstd = keep.tile([P, 1], F32)

        nc.vector.memset(b1_given[:].bitcast(I32), 0)
        nc.vector.memset(w1_scales_given[:].bitcast(I32), 0)
        nc.vector.memset(b2_rows[:].bitcast(I32), 0)
        nc.vector.memset(w2_scales[:].bitcast(I32), 0)
        nc.vector.memset(t_sums[:], 0.0)
        nc.vector.memset(ones_bf[:], 1.0)
        nc.vector.memset(eps[:], EPS)
        nc.vector.memset(mean_weights[:], 1.0 / (TOKENS * D_MODEL))
        make_identity(nc, identity[:])
        make_identity(nc, identity_bf[:])
        nc.scalar.activation(out=table_warmer[:], in_=eps[:], func=ACT.Abs_reciprocal_sqrt)

        def load_h(pair):
            tiles = block(pair, PAIR)
            nc.sync.dma_start(out=h_sb[:, tiles, :], in_=h_rows[:, tiles, :])

        load_h(0)
        load_h(1)
        nc.sync.dma_start(
            out=b1_given[0:N_GROUPS, :], in_=b_ff1.rearrange("(g f) -> g f", f=K_PASS)
        )
        for quad in range(QUADS):
            nc.sync.dma_start(
                out=w1_scales_given[32 * quad : 32 * quad + 16, :].bitcast(I32),
                in_=w_ff1_scales[0, 4 * quad : 4 * quad + 4, :]
                .bitcast(I32)
                .rearrange("r (g n) -> g r n", g=N_GROUPS),
            )
        w1_dram = w_ff1_words[0].rearrange("p n t -> p (n t)").bitcast(I32)

        def load_w1_words(g):
            nc.sync.dma_start(
                out=w1_words_given[:, block(g, K_PASS)].bitcast(I32),
                in_=w1_dram[:, block(g, K_PASS)],
            )

        load_w1_words(0)
        nc.sync.dma_start(out=b2_rows[0:1, :], in_=b_ff2.rearrange("(o n) -> o n", o=1))
        for g in range(1, N_GROUPS):
            load_w1_words(g)
        load_h(2)
        load_h(3)
        for quad in range(QUADS):
            nc.sync.dma_start(
                out=w2_scales[32 * quad : 32 * quad + 16, :].bitcast(I32),
                in_=w_ff2_scales[:, 4 * quad : 4 * quad + 4, :].bitcast(I32),
            )
        for g in range(N_GROUPS):
            nc.sync.dma_start(
                out=w2_words[:, g, :].bitcast(I32),
                in_=w_ff2_words[g].rearrange("p n t -> p (n t)").bitcast(I32),
            )

        planes_of = {}
        grouped_of = {}
        quantised_of = {}
        sums_of = {}

        def turn_h(pair):
            bank = psum_s.tile([P, 2, PAIR * P], F32, name="h_bank", tag="shared")
            for j in range(PAIR):
                words = h_sb[:, PAIR * pair + j, :].bitcast(F32)
                for u in range(2):
                    nc.tensor.transpose(
                        bank[:, u, block(j, P)], words[:, u : D_MODEL // 2 : 2], identity[:]
                    )
            copy = nc.scalar.copy if pair in SCALAR_TURNS else nc.vector.tensor_copy
            copy(
                out=h_grouped[:, block(pair, PAIR * K_PASS)]
                .bitcast(F32)
                .rearrange("p (c u) -> p c u", u=2),
                in_=bank[:].rearrange("p u c -> p c u"),
            )

        def quantise_h(pair):
            nc.vector.quantize_mx(
                out=h_words[:, block(pair, PAIR * P)].bitcast(FP8X4),
                scales=h_scales[:, block(pair, PAIR * P)],
                in_=h_grouped[:, block(pair, PAIR * K_PASS)],
            )

        def sort_w1_words(g):
            nc.vector.tensor_copy(
                out=w1_words[:, block(g, K_PASS)].bitcast(I32).rearrange("p (t m) -> p m t", t=PACK),
                in_=w1_words_given[:, block(g, K_PASS)].bitcast(I32).rearrange("p (m t) -> p m t", t=PACK),
            )

        def first_matmul(unit):
            first, tokens, g = UNITS[unit]
            columns = slice(first, first + tokens)
            a_planes = ring3.tile([P, PACK, tokens], BF16, name="a_planes")
            for t in range(PACK):
                j = PACK * g + t
                x = psum_x.tile([P, tokens], F32, name="x")
                nc.tensor.matmul_mx(
                    out=x[:],
                    lhsT=w1_words[:, block(j, P)].bitcast(FP8X4),
                    lhsT_scale=w1_scales[4 * g : P, block(t, P)],
                    rhs=h_words[:, columns].bitcast(FP8X4),
                    rhs_scale=h_scales[:, columns],
                    start=True,
                    stop=True,
                )
                if (unit, t) in VECTOR_TAKES:
                    nc.vector.tensor_scalar(
                        out=a_planes[:, t, :],
                        in0=x[:],
                        scalar1=b1_cols[:, j : j + 1],
                        scalar2=0.0,
                        op0=ALU.add,
                        op1=ALU.max,
                    )
                else:
                    nc.scalar.activation(
                        out=a_planes[:, t, :], in_=x[:], func=ACT.Relu, bias=b1_cols[:, j : j + 1]
                    )
            planes_of[unit] = a_planes

        def regroup_a(unit):
            tokens = UNITS[unit][1]
            grouped = ring3.tile([P, PACK * tokens], BF16, name="grouped", align_bytes=64)
            nc.vector.tensor_copy(
                out=grouped[:].rearrange("p (c i t) -> p c t i", i=4, t=PACK),
                in_=planes_of[unit][:].rearrange("p t (c i) -> p c t i", i=4),
            )
            grouped_of[unit] = grouped

        def quantise_a(unit):
            tokens = UNITS[unit][1]
            a_words = ring4.tile([P, tokens], U32, name="a_words", align_bytes=64)
            a_scales = ring4.tile([P, tokens], U8, name="a_scales", align_bytes=64)
            nc.vector.quantize_mx(
                out=a_words[:].bitcast(FP8X4), scales=a_scales[:], in_=grouped_of[unit][:]
            )
            quantised_of[unit] = (a_words, a_scales)

        def second_matmul(unit):
            first, tokens, g = UNITS[unit]
            a_words, a_scales = quantised_of[unit]
            for k in range(tokens // P):
                i = first // P + k
                if g == 0:
                    sums_of[i] = psum_s.tile([P, D_MODEL], F32, name="ff", tag="shared")
                nc.tensor.matmul_mx(
                    out=sums_of[i][:],
                    lhsT=a_words[:, block(k, P)].bitcast(FP8X4),
                    lhsT_scale=a_scales[:, block(k, P)],
                    rhs=w2_words[:, g, :].bitcast(FP8X4),
                    rhs_scale=w2_scales[4 * g : P, :],
                    start=(g == 0),
                    stop=(g == N_GROUPS - 1),
                )

        def add_residual(i):
            nc.vector.scalar_tensor_tensor(
                out=t_sb[:, i, :],
                in0=sums_of[i][:],
                scalar=1.0,
                in1=h_plus_b2[:, i, :],
                op0=ALU.mult,
                op1=ALU.add,
                accum_out=t_sums[:, 0, i : i + 1],
            )

        def sum_squares(i):
            nc.scalar.activation(
                out=squares[:, 0:D_MODEL],
                in_=t_sb[:, i, :],
                func=ACT.Square,
                accum_out=t_sums[:, 1, i : i + 1],
            )

        nc.vector.tensor_copy(
            out=b1_sorted[:].rearrange(SORTED, t=PACK),
            in_=b1_given[:].rearrange(AS_GIVEN, t=PACK),
        )
        nc.vector.tensor_copy(
            out=w1_scales[:].rearrange(SORTED, t=PACK),
            in_=w1_scales_given[:].rearrange(AS_GIVEN, t=PACK),
        )
        turn_h(0)
        quantise_h(0)
        sort_w1_words(0)
        turn_h(1)
        quantise_h(1)
        b1_bank = psum_s.tile([P, PACK, P], BF16, name="b1_bank", tag="shared")
        for t in range(PACK):
            nc.tensor.transpose(b1_bank[:, t, :], b1_sorted[:, block(t, P)], identity_bf[:])
        nc.vector.tensor_copy(
            out=b1_cols[:].rearrange("p (g t) -> p t g", t=PACK), in_=b1_bank[:, :, 0:N_GROUPS]
        )
        def add_b2(i):
            bank = psum_x.tile([P, D_MODEL], F32, name="x")
            nc.tensor.matmul(
                out=bank[:], lhsT=identity_bf[:], rhs=h_sb[:, i, :], start=True, stop=False
            )
            nc.tensor.matmul(out=bank[:], lhsT=ones_bf[:], rhs=b2_rows[:], start=False, stop=True)
            nc.scalar.copy(out=h_plus_b2[:, i, :], in_=bank[:])

        def spread_b2():
            bank = psum_x.tile([P, D_MODEL], F32, name="x")
            nc.tensor.matmul(out=bank[:], lhsT=ones_bf[:], rhs=b2_rows[:], start=True, stop=True)
            nc.scalar.copy(out=b2_all[:], in_=bank[:])

        def add_b2_on_vector(i):
            nc.vector.tensor_tensor(
                out=h_plus_b2[:, i, :], in0=h_sb[:, i, :], in1=b2_all[:], op=ALU.add
            )

        def sum_squares_of_two(i):
            nc.scalar.activation(
                out=squares[:],
                in_=t_sb[:, i : i + 2, :].rearrange("p i d -> p (i d)"),
                func=ACT.Square,
                accum_out=t_sums[:, 1, i : i + 1],
            )

        for step in PLAN:
            job, arg = step
            if job == "first":
                first_matmul(arg)
            elif job == "sort":
                sort_w1_words(arg)
            elif job == "ht":
                turn_h(arg)
            elif job == "hq":
                quantise_h(arg)
            elif job == "hb":
                add_b2(arg)
            elif job == "regroup":
                regroup_a(arg)
            elif job == "quantise":
                quantise_a(arg)
            elif job == "second":
                second_matmul(arg)
            elif job == "t":
                add_residual(arg)
            elif job == "sq":
                sum_squares(arg)
            elif job == "sq2":
                sum_squares_of_two(arg)
            elif job == "b2":
                spread_b2()
            elif job == "hbv":
                add_b2_on_vector(arg)

        totals = psum_s.tile([P, 2], F32, name="totals", tag="shared")
        for i in range(N_TILES):
            nc.tensor.matmul(
                out=totals[:],
                lhsT=mean_weights[:],
                rhs=t_sums[:, :, i],
                start=(i == 0),
                stop=(i == N_TILES - 1),
            )
        nc.vector.tensor_copy(out=mean[:], in_=totals[:, 0:1])
        nc.vector.tensor_scalar(
            out=minus_var[:],
            in0=totals[:, 0:1],
            scalar1=totals[:, 0:1],
            scalar2=totals[:, 1:2],
            op0=ALU.mult,
            op1=ALU.subtract,
        )
        nc.scalar.activation(
            out=rstd[:], in_=minus_var[:], func=ACT.Abs_reciprocal_sqrt, scale=-1.0, bias=eps[:]
        )
        first_of_store = 0
        for n, tiles in enumerate(STORE_TILES):
            for i in range(first_of_store, first_of_store + tiles):
                nc.vector.tensor_scalar(
                    out=t_sb[:, i, :],
                    in0=t_sb[:, i, :],
                    scalar1=mean[:],
                    scalar2=rstd[:],
                    op0=ALU.subtract,
                    op1=ALU.mult,
                )
            stored = slice(first_of_store, first_of_store + tiles)
            queue = nc.sync if n % 2 == 0 else nc.scalar
            queue.dma_start(out=out_rows[:, stored, :], in_=t_sb[:, stored, :])
            first_of_store += tiles
